import numpy as np
import ml_dtypes


def mxq(x, axis, fmt="e4m3"):
    dtype, down = {"e4m3": (ml_dtypes.float8_e4m3fn, 7), "e5m2": (ml_dtypes.float8_e5m2, 14)}[fmt]
    v = np.moveaxis(np.asarray(x, np.float32).astype(ml_dtypes.bfloat16).astype(np.float64), axis, -1)
    blocks = v.reshape(v.shape[:-1] + (-1, 32))
    amax = np.abs(blocks).max(-1, keepdims=True)
    byte = np.maximum(np.where(amax > 0, np.frexp(amax)[1] - 1 + 127, 0) - down, 1)
    scale = np.exp2(byte - 127.0)
    codes = (blocks / scale).astype(np.float32).astype(dtype).astype(np.float64)
    return np.moveaxis((codes * scale).reshape(v.shape), -1, axis)


WIDE = False


def mx_kscale(k):
    if not WIDE:
        return np.ones(k)
    levels = np.array([10, -10, 5, -5, 0])
    if k % 512:
        return np.exp2(np.random.permutation(np.resize(levels, k // 32))).repeat(32)
    a = np.empty((k // 512, 16))
    for p in range(k // 512):
        a[p, :8] = np.random.permutation(np.resize(levels, 8))
        for g in range(8):
            far = levels[np.abs(levels - a[p, g]) >= 10]
            a[p, g + 8] = far[np.random.randint(len(far))]
    return np.exp2(a.ravel()).repeat(32)


BF16 = ml_dtypes.bfloat16


def bf(x):
    return np.asarray(x, np.float32).astype(BF16)


def f64(x):
    return np.asarray(x).astype(np.float64)


B, I, HS, G = 8192, 1024, 128, 1
H = HS * G
MXK = 16 * 32
HH_MX = H % MXK == 0


def sigmoid(v):
    return 1.0 / (1.0 + np.exp(-v))


def setup_inputs():
    s = mx_kscale(I)
    t = mx_kscale(H) if HH_MX else np.ones(H)
    return {"input": bf(np.random.standard_normal((B, I)) * s),
            "h0": bf(np.random.standard_normal((B, H)) * t),
            "c0": bf(np.random.standard_normal((B, H))),
            "weight_ih": bf(np.random.standard_normal((I, 4 * H)) * 0.7 / np.sqrt(I) / s[:, None]),
            "weight_hh": bf(np.random.standard_normal((H, 4 * H)) * 0.7 / np.sqrt(H) / t[:, None]),
            "bias_ih": bf(np.random.standard_normal(4 * H) * 0.3),
            "bias_hh": bf(np.random.standard_normal(4 * H) * 0.3)}


def reference(input, h0, c0, weight_ih, weight_hh, bias_ih, bias_hh):
    pi = mxq(f64(input), 1, "e4m3") @ mxq(f64(weight_ih), 0, "e4m3")
    if HH_MX:
        ph = mxq(f64(h0), 1, "e4m3") @ mxq(f64(weight_hh), 0, "e4m3")
    else:
        ph = f64(h0) @ f64(weight_hh)
    gates = pi + f64(bias_ih) + ph + f64(bias_hh)
    c_in = f64(c0)
    h_parts, c_parts = [], []
    st = 0
    for _ in range(G):
        blk = gates[:, st * 4: st * 4 + 4 * HS]
        g, i, f, o = np.split(blk, 4, axis=-1)
        c1 = np.tanh(g) * sigmoid(i) + c_in[:, st: st + HS] * sigmoid(f)
        h_parts.append(np.tanh(c1) * sigmoid(o))
        c_parts.append(c1)
        st += HS
    return np.concatenate(h_parts, axis=-1), np.concatenate(c_parts, axis=-1)

@@ -1,0 +1,383 @@
+from contextlib import ExitStack
+
+import concourse.mybir as mybir
+from concourse.masks import make_identity
+
+F32 = mybir.dt.float32
+BF16 = mybir.dt.bfloat16
+U32 = mybir.dt.uint32
+U8 = mybir.dt.uint8
+FP8X4 = mybir.dt.float8_e4m3fn_x4
+ACT = mybir.ActivationFunctionType
+ALU = mybir.AluOpType
+
+P = 128
+BATCH = 8192
+K_IN = 1024
+HID = 128
+GATES = 512
+NT = BATCH // P
+GT = 2
+NG = NT // GT
+XC = 4
+XB = 4
+LEAD = 8
+SB_SET = (3,)
+SB_MOD = 4
+SMALL = ("g", "g", "g", "v")
+SMALL_TAIL = ("v", "v", "v", "v")
+TAILB = 2
+EB = 2
+LINKB = 2
+KH = 1
+KT = 13
+HEAD = [
+    [("H", 0), ("P", 1), ("P", 0), ("T", 1), ("T", 2), ("T", 0), ("P", 2), ("T", 3), ("P", 3), ("H", 1), ("T", 5), ("T", 4), ("P", 4), ("P", 5), ("T", 7), ("T", 6), ("M", 0), ("P", 6), ("T", 8), ("T", 10), ("P", 7), ("M", 1), ("P", 8), ("T", 9), ("T", 11), ("P", 9), ("M", 2), ("M", 3), ("P", 11), ("P", 10)],
+    [("B", 0), ("B", 1), ("W", 0), ("W", 3), ("W", 2), ("B", 2), ("Q", 0), ("B", 4), ("B", 5), ("A", 0), ("B", 6), ("Q", 1), ("A", 1), ("B", 8), ("B", 9), ("A", 2), ("A", 3), ("B", 10)],
+    [("HC", 0), ("W", 1), ("E", 1), ("E", 2), ("E", 0), ("E", 3), ("B", 3), ("HC", 1), ("E", 5), ("E", 4), ("E", 7), ("E", 6), ("B", 7), ("E", 10), ("E", 8), ("E", 9), ("E", 11), ("S1", 0), ("B", 11)],
+    [],
+]
+TAIL = [
+    [("T", 61), ("M", 52), ("P", 60), ("P", 61), ("T", 62), ("M", 53), ("T", 60), ("T", 63), ("M", 54), ("M", 55), ("M", 56), ("M", 57), ("M", 58), ("M", 59), ("P", 62), ("M", 60), ("M", 61), ("P", 63), ("M", 62), ("M", 63)],
+    [("G2", 10), ("Q", 14), ("A", 52), ("B", 60), ("A", 53), ("A", 54), ("B", 61), ("A", 55), ("G2", 11), ("Q", 15), ("A", 56), ("A", 57), ("A", 58), ("A", 59), ("G2", 12), ("A", 61), ("A", 60), ("B", 62), ("A", 62), ("A", 63), ("G1", 15), ("C1", 15), ("G2", 13), ("G1", 16), ("C1", 16), ("G2", 14), ("G2", 15), ("G2", 16)],
+    [("S1", 25), ("S2", 11), ("E", 61), ("E", 62), ("E", 60), ("E", 63), ("S1", 26), ("S1", 27), ("S2", 12), ("S1", 28), ("S1", 29), ("S2", 13), ("B", 63), ("S1", 30), ("S1", 31), ("S2", 14), ("S2", 15), ("S2", 16)],
+    [("G1", 12), ("C1", 12), ("G1", 13), ("C1", 13), ("G1", 14), ("C1", 14)],
+]
+PE_ORDER = [("H", 3, 0), ("M", 0, 0), ("M", 0, 1), ("P", 2, 0), ("T", 2, 1), ("T", 2, 0), ("P", 2, 1), ("T", 2, 2), ("T", 2, 3), ("M", 0, 2), ("M", 0, 3), ("P", 2, 2), ("P", 2, 3)]
+V_ORDER = [("G2", -3, 0), ("W", -2, 2), ("Q", 1, 0), ("A", 0, 0), ("A", 0, 1), ("B", 2, 0), ("B", 2, 1), ("A", 0, 2), ("W", -1, 3), ("B", 1, 3), ("A", 0, 3), ("B", 2, 2), ("W", -3, 0)]
+S_ORDER = [("S1", -1, 1), ("HC", 3, 0), ("S2", -2, 0), ("W", -2, 1), ("E", 2, 1), ("E", 2, 0), ("E", 2, 2), ("S1", 0, 0), ("E", 2, 3), ("B", 2, 3)]
+G_ORDER = [("G1", -1, 0), ("C1", -1, 0)]
+
+FLOPS = 2 * BATCH * K_IN * GATES + 2 * BATCH * HID * GATES
+
+
+def tile_symlstmcell_t_kernel(tc, x, h0, c0, weight_ih, weight_hh, bias_ih, bias_hh, out_0, out_1):
+    nc = tc.nc
+    xv = x.rearrange("(p t) k -> p t k", t=NT)
+    h0v = h0.rearrange("(p t) k -> p t k", t=NT)
+    c0v = c0.rearrange("(p t) k -> p t k", t=NT)
+    h1v = out_0.rearrange("(p t) u -> p t u", t=NT)
+    c1v = out_1.rearrange("(p t) u -> p t u", t=NT)
+
+    with ExitStack() as ctx:
+        const = ctx.enter_context(tc.tile_pool(name="const", bufs=1))
+        xpool = ctx.enter_context(tc.tile_pool(name="xpool", bufs=XB))
+        gpool = ctx.enter_context(tc.tile_pool(name="gpool", bufs=2))
+        qpool = ctx.enter_context(tc.tile_pool(name="qpool", bufs=3))
+        tpool = ctx.enter_context(tc.tile_pool(name="tpool", bufs=LEAD))
+        apool = ctx.enter_context(tc.tile_pool(name="apool", bufs=4))
+        opool = ctx.enter_context(tc.tile_pool(name="opool", bufs=4))
+        lpool = ctx.enter_context(tc.tile_pool(name="lpool", bufs=1))
+        hpool = ctx.enter_context(tc.tile_pool(name="hpool", bufs=3))
+        ps_x = ctx.enter_context(tc.psum_pool(name="ps_x", bufs=4))
+        ps_g = ctx.enter_context(tc.psum_pool(name="ps_g", bufs=2))
+        ps_p = ctx.enter_context(tc.psum_pool(name="ps_p", bufs=2))
+        ctx.enter_context(tc.manual_schedule())
+
+        eng = {"v": nc.vector, "g": nc.gpsimd}
+
+        ident_f = const.tile([P, P], F32, name="ident_f")
+        ident_b = const.tile([P, P], BF16, name="ident_b")
+        make_identity(nc, ident_b[:])
+        make_identity(nc, ident_f[:])
+        btile = const.tile([P, GATES], BF16, name="btile")
+        nc.vector.memset(btile[:], 0.0)
+        ones = const.tile([P, P], BF16, name="ones")
+        nc.vector.memset(ones[:], 1.0)
+        warm = const.tile([P, 1], F32, name="warm")
+        nc.vector.memset(warm[:], 0.0)
+
+        nc.sync.dma_start(out=btile[0:1, :], in_=bias_ih.rearrange("(o n) -> o n", o=1))
+        nc.scalar.dma_start(out=btile[1:2, :], in_=bias_hh.rearrange("(o n) -> o n", o=1))
+        nc.scalar.activation(out=warm[:], in_=warm[:], func=ACT.Sigmoid)
+
+        h0_parts = []
+        c0_parts = []
+
+        def load_part(parts, view, lo, hi, nm):
+            part = const.tile([P, hi - lo, HID], BF16, name="%s%d" % (nm, lo))
+            nc.sync.dma_start(out=part[:], in_=view[:, lo:hi, :])
+            parts.append((lo, hi, part))
+
+        def part_of(parts, lo, n):
+            found = [(a, part) for (a, b, part) in parts if a <= lo and lo + n <= b]
+            assert len(found) == 1
+            a, part = found[0]
+            return part[:, lo - a:lo - a + n, :]
+
+        xs = {}
+
+        def load_x(c):
+            xc = xpool.tile([P, XC, K_IN], BF16, name="xc")
+            nc.sync.dma_start(out=xc[:], in_=xv[:, XC * c:XC * (c + 1), :])
+            xs[c] = xc
+
+        load_part(h0_parts, h0v, 0, 16, "h0p")
+        whh = const.tile([P, GATES], BF16, name="whh")
+        nc.sync.dma_start(out=whh[:], in_=weight_hh)
+        w_raw = const.tile([P, 4 * K_IN], BF16, name="w_raw")
+        nc.sync.dma_start(
+            out=w_raw[:].rearrange("p (g r) -> p g r", g=2),
+            in_=weight_ih.rearrange("(g q j) c -> q g (j c)", g=2, j=4),
+        )
+        load_x(0)
+        load_x(1)
+        load_part(c0_parts, c0v, 0, 16, "c0p")
+        load_x(2)
+        load_part(h0_parts, h0v, 16, NT, "h0p")
+        load_x(3)
+        load_part(c0_parts, c0v, 16, NT, "c0p")
+        for c in range(4, XB):
+            load_x(c)
+
+        hT = {}
+        h0ts = {}
+        xts = {}
+        grps = {}
+        cods = {}
+        scls = {}
+        ppss = {}
+        gpss = {}
+        tmps = {}
+        acts = {}
+        c1os = {}
+        tcbs = {}
+        NQ = NT // 4
+
+        batches = []
+        j0 = 0
+        while j0 < NG:
+            n = EB if j0 + EB <= NG - TAILB else 1
+            batches.append((j0, n, SMALL if n == EB else SMALL_TAIL))
+            j0 += n
+        batch_of = {}
+        for bi, (bj, bn, be) in enumerate(batches):
+            for j in range(bj, bj + bn):
+                batch_of[j] = bi
+        n_full = len([b for b in batches if b[1] == EB])
+
+        def on_scalar(t):
+            return t % SB_MOD in SB_SET
+
+        def st_H(b):
+            h0t = ps_x.tile([P, 8, HID], BF16, name="xt")
+            blk = part_of(h0_parts, 8 * b, 8)
+            for i in range(8):
+                nc.tensor.transpose(h0t[:, i, :], blk[:, i, :], ident_b[:])
+            h0ts[b] = h0t
+
+        def st_HC(b):
+            ht = hpool.tile([P, 8, HID], BF16, name="ht")
+            nc.scalar.copy(out=ht[:], in_=h0ts[b][:])
+            hT[b] = ht
+
+        def st_P(t):
+            pps = ps_p.tile([P, GATES], F32, name="pps")
+            sc = on_scalar(t)
+            nc.tensor.matmul(out=pps[:], lhsT=hT[t // 8][:, t % 8, :], rhs=whh[:], start=True, stop=not sc)
+            if sc:
+                nc.tensor.matmul(out=pps[:], lhsT=ones[:], rhs=btile[:], start=False, stop=True)
+            ppss[t] = pps
+
+        def st_B(t):
+            if t // GT not in tmps:
+                tmp = tpool.tile([P, GT, GATES], F32, name="tmp")
+                tmps[t // GT] = tmp
+            dst = tmps[t // GT][:, t % GT, :]
+            if on_scalar(t):
+                nc.scalar.copy(out=dst, in_=ppss[t][:])
+            else:
+                nc.vector.tensor_tensor(out=dst, in0=ppss[t][:], in1=bias_bc[:], op=ALU.add)
+
+        def st_T(t):
+            xt = ps_x.tile([P, 4, P], F32, name="xt")
+            xw = xs[t // XC][:, t % XC, :].bitcast(F32)
+            for u in range(4):
+                lo = 2 * P * (u // 2) + u % 2
+                nc.tensor.transpose(xt[:, u, :], xw[:, lo:lo + 2 * P - 1:2], ident_f[:])
+            xts[t] = xt
+            if t % XC == XC - 1 and t // XC + XB < NT // XC:
+                load_x(t // XC + XB)
+
+        def st_E(t):
+            q = t // 4
+            if q not in grps:
+                grp = gpool.tile([P, 4, K_IN], BF16, name="grp", align_bytes=64)
+                grps[q] = grp
+            nc.scalar.copy(
+                out=grps[q][:, t % 4, :].bitcast(F32).rearrange("p (g b u) -> p g b u", g=2, u=2),
+                in_=xts[t][:].rearrange("p (g u) b -> p g b u", u=2),
+            )
+
+        def st_Q(q):
+            cod = qpool.tile([P, 4 * 256], U32, name="cod", align_bytes=64)
+            scl = qpool.tile([P, 4 * 256], U8, name="scl", align_bytes=64)
+            nc.vector.quantize_mx(
+                out=cod[:].bitcast(FP8X4), scales=scl[:], in_=grps[q][:].rearrange("p j c -> p (j c)")
+            )
+            cods[q] = cod
+            scls[q] = scl
+
+        def st_M(t):
+            gps = ps_g.tile([P, GATES], F32, name="gps")
+            for g in range(2):
+                lo = (t % 4) * 256 + g * P
+                nc.tensor.matmul_mx(
+                    out=gps[:],
+                    lhsT=cods[t // 4][:, lo:lo + P].bitcast(FP8X4),
+                    lhsT_scale=scls[t // 4][:, lo:lo + P],
+                    rhs=wq[:, g, :].bitcast(FP8X4),
+                    rhs_scale=ws[:, g, :],
+                    start=(g == 0),
+                    stop=(g == 1),
+                )
+            gpss[t] = gps
+
+        def st_A(t):
+            dst = tmps[t // GT][:, t % GT, :]
+            nc.vector.tensor_tensor(out=dst, in0=gpss[t][:], in1=dst, op=ALU.add)
+
+        def st_S1(j):
+            bi = batch_of[j]
+            bj, bn, be = batches[bi]
+            if bi not in acts:
+                act = apool.tile([P, bn * GT, GATES], F32, name="act")
+                acts[bi] = act
+            lo = (j - bj) * GT
+            act = acts[bi][:, lo:lo + GT, :]
+            nc.scalar.activation(out=act[:, :, HID:GATES], in_=tmps[j][:, :, HID:GATES], func=ACT.Sigmoid)
+            nc.scalar.activation(out=act[:, :, 0:HID], in_=tmps[j][:, :, 0:HID], func=ACT.Tanh)
+
+        def st_G1(bi):
+            bj, bn, be = batches[bi]
+            act = acts[bi]
+            if bn == EB:
+                m1 = lpool.tile([P, bn * GT, HID], F32, name="lk", bufs=LINKB)
+            else:
+                m1 = lpool.tile([P, bn * GT, HID], F32, name="lkt", bufs=2)
+            tcbs[bi] = m1
+            eng[be[0]].tensor_tensor(out=m1[:], in0=act[:, :, 0:HID], in1=act[:, :, HID:2 * HID], op=ALU.mult)
+            eng[be[1]].tensor_tensor(
+                out=act[:, :, 2 * HID:3 * HID], in0=act[:, :, 2 * HID:3 * HID],
+                in1=part_of(c0_parts, GT * bj, GT * bn), op=ALU.mult
+            )
+
+        def st_C1(bi):
+            bj, bn, be = batches[bi]
+            c1o = opool.tile([P, bn * GT, HID], F32, name="c1o")
+            c1os[bi] = c1o
+            eng[be[2]].tensor_tensor(out=c1o[:], in0=tcbs[bi][:], in1=acts[bi][:, :, 2 * HID:3 * HID], op=ALU.add)
+            nc.sync.dma_start(out=c1v[:, GT * bj:GT * (bj + bn), :], in_=c1o[:])
+
+        def st_S2(bi):
+            nc.scalar.activation(out=tcbs[bi][:], in_=c1os[bi][:], func=ACT.Tanh)
+
+        def st_G2(bi):
+            bj, bn, be = batches[bi]
+            h1o = opool.tile([P, bn * GT, HID], F32, name="h1o")
+            eng[be[3]].tensor_tensor(out=h1o[:], in0=tcbs[bi][:], in1=acts[bi][:, :, 3 * HID:GATES], op=ALU.mult)
+            nc.sync.dma_start(out=h1v[:, GT * bj:GT * (bj + bn), :], in_=h1o[:])
+
+        bps = ps_p.tile([P, GATES], F32, name="pps")
+        nc.tensor.matmul(out=bps[:], lhsT=ones[:], rhs=btile[:], start=True, stop=True)
+        bias_bc = const.tile([P, GATES], F32, name="bias_bc")
+        nc.vector.tensor_copy(out=bias_bc[:], in_=bps[:])
+        wview = w_raw[:].rearrange("p (g t c) -> p g t c", g=2, t=4)
+        wq = const.tile([P, 2, GATES], U32, name="wq", align_bytes=64)
+        ws = const.tile([P, 2, GATES], U8, name="ws", align_bytes=64)
+        wg0 = const.tile([P, GATES, 4], BF16, name="wg0", align_bytes=64)
+        wg1 = const.tile([P, GATES, 4], BF16, name="wg1", align_bytes=64)
+
+        def st_W(i):
+            if i == 0:
+                nc.vector.tensor_copy(
+                    out=wg0[:].rearrange("p (c i) t -> p c t i", i=4), in_=wview[:, 0].rearrange("p t (c i) -> p c t i", i=4)
+                )
+            elif i == 1:
+                nc.scalar.copy(
+                    out=wg1[:].rearrange("p (c i) t -> p c t i", i=4), in_=wview[:, 1].rearrange("p t (c i) -> p c t i", i=4)
+                )
+            elif i == 2:
+                nc.vector.quantize_mx(out=wq[:, 0, :].bitcast(FP8X4), scales=ws[:, 0, :], in_=wg0[:].rearrange("p c t -> p (c t)"))
+            else:
+                nc.vector.quantize_mx(out=wq[:, 1, :].bitcast(FP8X4), scales=ws[:, 1, :], in_=wg1[:].rearrange("p c t -> p (c t)"))
+
+        def needs(s, i):
+            if s == "E":
+                return [("T", i)]
+            if s == "Q":
+                return [("E", 4 * i + r) for r in range(4)]
+            if s == "M":
+                return [("Q", i // 4), ("W", 2), ("W", 3)]
+            if s == "W":
+                return [("W", i - 2)] if i >= 2 else []
+            if s == "A":
+                return [("M", i), ("B", i)]
+            if s == "B":
+                return [("P", i)]
+            if s == "P":
+                return [("HC", i // 8)]
+            if s == "HC":
+                return [("H", i)]
+            if s == "S1":
+                return [("A", GT * i), ("A", GT * i + 1)]
+            if s == "G1":
+                bj, bn, be = batches[i]
+                old = [("G2", i - LINKB)] if (bn == EB and i >= LINKB) else []
+                return [("S1", j) for j in range(bj, bj + bn)] + old
+            if s == "C1":
+                return [("G1", i)]
+            if s == "S2":
+                return [("C1", i)]
+            if s == "G2":
+                return [("S2", i)]
+            return []
+
+        count = {"T": NT, "E": NT, "Q": NQ, "M": NT, "A": NT, "B": NT, "P": NT, "H": NT // 8, "HC": NT // 8,
+                 "S1": NG, "G1": n_full, "C1": n_full, "S2": n_full, "G2": n_full, "W": 4}
+        per = {"T": 4, "E": 4, "Q": 1, "M": 4, "A": 4, "B": 4, "P": 4, "S1": 2, "G1": 1, "C1": 1, "S2": 1, "G2": 1}
+        run = {"T": st_T, "E": st_E, "Q": st_Q, "M": st_M, "A": st_A, "B": st_B, "P": st_P, "H": st_H, "HC": st_HC,
+               "S1": st_S1, "G1": st_G1, "C1": st_C1, "S2": st_S2, "G2": st_G2, "W": st_W}
+
+        def expand(order, mine):
+            out = []
+            for k in range(KH, KT):
+                for (s, ahead, r) in order:
+                    if s == "W":
+                        if k == ahead:
+                            out.append((s, r))
+                        continue
+                    if s == "H" or s == "HC":
+                        if (k + ahead) % 2 == r and 0 <= (k + ahead) // 2 < count[s]:
+                            out.append((s, (k + ahead) // 2))
+                        continue
+                    i = per[s] * (k + ahead) + r
+                    if 0 <= k + ahead and 0 <= i < count[s] and mine(s, i):
+                        if s == "S1" and batches[batch_of[i]][1] != EB:
+                            continue
+                        out.append((s, i))
+            return out
+
+        lists = [
+            HEAD[0] + expand(PE_ORDER, lambda s, i: True) + TAIL[0],
+            HEAD[1] + expand(V_ORDER, lambda s, i: s != "B" or not on_scalar(i)) + TAIL[1],
+            HEAD[2] + expand(S_ORDER, lambda s, i: s != "B" or on_scalar(i)) + TAIL[2],
+            HEAD[3] + expand(G_ORDER, lambda s, i: True) + TAIL[3],
+        ]
+
+        done = set()
+        pos = [0, 0, 0, 0]
+        left = sum([len(li) for li in lists])
+        while left > 0:
+            moved = False
+            for e in range(4):
+                while pos[e] < len(lists[e]):
+                    s, i = lists[e][pos[e]]
+                    if not all([d in done for d in needs(s, i)]):
+                        break
+                    run[s](i)
+                    done.add((s, i))
+                    pos[e] += 1
+                    left -= 1
+                    moved = True
+            assert moved, "the orders wait for each other"

@@ -17,38 +17,68 @@ K_IN = 1024
 HID = 128
 GATES = 512
 NT = BATCH // P
-GT = 2
-NG = NT // GT
-XC = 4
-XB = 4
-LEAD = 8
-SB_SET = (3,)
-SB_MOD = 4
-SMALL = ("g", "g", "g", "v")
-SMALL_TAIL = ("v", "v", "v", "v")
-TAILB = 2
-EB = 2
-LINKB = 2
-KH = 1
-KT = 13
-HEAD = [
-    [("H", 0), ("P", 1), ("P", 0), ("T", 1), ("T", 2), ("T", 0), ("P", 2), ("T", 3), ("P", 3), ("H", 1), ("T", 5), ("T", 4), ("P", 4), ("P", 5), ("T", 7), ("T", 6), ("M", 0), ("P", 6), ("T", 8), ("T", 10), ("P", 7), ("M", 1), ("P", 8), ("T", 9), ("T", 11), ("P", 9), ("M", 2), ("M", 3), ("P", 11), ("P", 10)],
-    [("B", 0), ("B", 1), ("W", 0), ("W", 3), ("W", 2), ("B", 2), ("Q", 0), ("B", 4), ("B", 5), ("A", 0), ("B", 6), ("Q", 1), ("A", 1), ("B", 8), ("B", 9), ("A", 2), ("A", 3), ("B", 10)],
-    [("HC", 0), ("W", 1), ("E", 1), ("E", 2), ("E", 0), ("E", 3), ("B", 3), ("HC", 1), ("E", 5), ("E", 4), ("E", 7), ("E", 6), ("B", 7), ("E", 10), ("E", 8), ("E", 9), ("E", 11), ("S1", 0), ("B", 11)],
-    [],
-]
-TAIL = [
-    [("T", 61), ("M", 52), ("P", 60), ("P", 61), ("T", 62), ("M", 53), ("T", 60), ("T", 63), ("M", 54), ("M", 55), ("M", 56), ("M", 57), ("M", 58), ("M", 59), ("P", 62), ("M", 60), ("M", 61), ("P", 63), ("M", 62), ("M", 63)],
-    [("G2", 10), ("Q", 14), ("A", 52), ("B", 60), ("A", 53), ("A", 54), ("B", 61), ("A", 55), ("G2", 11), ("Q", 15), ("A", 56), ("A", 57), ("A", 58), ("A", 59), ("G2", 12), ("A", 61), ("A", 60), ("B", 62), ("A", 62), ("A", 63), ("G1", 15), ("C1", 15), ("G2", 13), ("G1", 16), ("C1", 16), ("G2", 14), ("G2", 15), ("G2", 16)],
-    [("S1", 25), ("S2", 11), ("E", 61), ("E", 62), ("E", 60), ("E", 63), ("S1", 26), ("S1", 27), ("S2", 12), ("S1", 28), ("S1", 29), ("S2", 13), ("B", 63), ("S1", 30), ("S1", 31), ("S2", 14), ("S2", 15), ("S2", 16)],
-    [("G1", 12), ("C1", 12), ("G1", 13), ("C1", 13), ("G1", 14), ("C1", 14)],
-]
-PE_ORDER = [("H", 3, 0), ("M", 0, 0), ("M", 0, 1), ("P", 2, 0), ("T", 2, 1), ("T", 2, 0), ("P", 2, 1), ("T", 2, 2), ("T", 2, 3), ("M", 0, 2), ("M", 0, 3), ("P", 2, 2), ("P", 2, 3)]
-V_ORDER = [("G2", -3, 0), ("W", -2, 2), ("Q", 1, 0), ("A", 0, 0), ("A", 0, 1), ("B", 2, 0), ("B", 2, 1), ("A", 0, 2), ("W", -1, 3), ("B", 1, 3), ("A", 0, 3), ("B", 2, 2), ("W", -3, 0)]
-S_ORDER = [("S1", -1, 1), ("HC", 3, 0), ("S2", -2, 0), ("W", -2, 1), ("E", 2, 1), ("E", 2, 0), ("E", 2, 2), ("S1", 0, 0), ("E", 2, 3), ("B", 2, 3)]
-G_ORDER = [("G1", -1, 0), ("C1", -1, 0)]
-
+NQ = NT // 4
 FLOPS = 2 * BATCH * K_IN * GATES + 2 * BATCH * HID * GATES
+
+XB = 4
+GRPB = 2
+CODB = 3
+TMPB = 10
+ACTB = 4
+HTB = 3
+X_BANKS, P_BANKS, G_BANKS = 4, 2, 2
+
+BATCHES = [(4 * q, 4) for q in range(NQ - 1)] + [(60, 2), (62, 1), (63, 1)]
+UNITS = [(2 * u, 2) for u in range(2 * NQ - 2)] + [(60, 2), (62, 1), (63, 1)]
+NB = NQ - 1
+NU = 2 * NQ - 2
+
+
+def t4(s, q):
+    return [(s, 4 * q + r) for r in range(4)]
+
+
+def on_scalar(t):
+    return t % 4 == 3
+
+
+tpl = {
+    "PE": [("M", 1, 2), ("M", 1, 3), ("P", 2, 3), ("M", 2, 0), ("M", 2, 1), ("P", 3, 0), ("T", 3, 3), ("P", 3, 1), ("H", 5, 0), ("T", 4, 0), ("T", 4, 1), ("T", 4, 2), ("P", 3, 2)],
+    "V": [("A", 1, 2), ("A", 1, 3), ("B", 2, 2), ("A", 2, 0), ("A", 2, 1), ("B", 3, 0), ("h1", -1, 0), ("Q", 3, 0), ("B", 3, 1)],
+    "S": [("S1", 1, 0), ("E", 3, 1), ("S2", -1, 0), ("HC", 4, 0), ("B", 2, 3), ("E", 3, 2), ("E", 3, 3), ("S1", 1, 1), ("E", 4, 0)],
+    "G": [("m1", 1, 0), ("cf", 1, 0), ("c1", 1, 0)],
+}
+head = {
+    "PE": [("H", 0), ("T", 0), ("P", 0), ("T", 1), ("P", 1), ("T", 2), ("P", 2), ("T", 3), ("H", 1), ("P", 3), ("T", 4), ("P", 4), ("T", 5), ("P", 5), ("M", 0), ("M", 1), ("T", 6), ("T", 7)],
+    "V": [("BB", 0), ("B", 0), ("B", 1), ("B", 2), ("W", 0), ("WQ", 0), ("Q", 0), ("B", 4), ("WQ", 1), ("A", 0), ("B", 5), ("Q", 1)],
+    "S": [("HC", 0)]+t4("E", 0)+[("HC", 1), ("B", 3), ("W", 1), ("E", 4), ("E", 5), ("E", 6), ("E", 7)],
+    "G": [],
+}
+tail = {
+    "PE": [],"V": [("cf", 14), ("m1", 15), ("cf", 15), ("c1", 14), ("c1", 15), ("m1", 16), ("cf", 16), ("h1", 14), ("c1", 16), ("h1", 15), ("m1", 17), ("cf", 17), ("c1", 17), ("h1", 16), ("h1", 17)],
+    "S": [("S1", 30), ("S1", 31), ("S2", 14), ("S1", 32), ("S2", 15), ("S2", 16), ("S2", 17)],"G": []
+}
+
+
+def engine_lists():
+    per = {"T": 4, "E": 4, "M": 4, "A": 4, "P": 4, "B": 4, "Q": 1, "S1": 2, "S2": 1, "m1": 1, "cf": 1, "c1": 1, "h1": 1, "H": 1, "HC": 1}
+    count = {"T": NT, "E": NT, "M": NT, "A": NT, "P": NT, "B": NT, "Q": NQ, "S1": NU, "S2": NB, "m1": NB, "cf": NB, "c1": NB, "h1": NB, "H": NQ, "HC": NQ}
+    placed = set()
+    for e in tpl:
+        placed = placed | set(head[e]) | set(tail[e])
+    lists = {}
+    for e in tpl:
+        lst = list(head[e])
+        for k in range(-8, NQ + 8):
+            for s, a, r in tpl[e]:
+                i = per[s] * (k + a) + r
+                if k + a < 0 or i >= count[s] or (s, i) in placed:
+                    continue
+                if s == "B" and (e == "S") != on_scalar(i):
+                    continue
+                lst.append((s, i))
+        lists[e] = lst + tail[e]
+    return lists
 
 
 def tile_symlstmcell_t_kernel(tc, x, h0, c0, weight_ih, weight_hh, bias_ih, bias_hh, out_0, out_1):
@@ -62,37 +92,21 @@ def tile_symlstmcell_t_kernel(tc, x, h0, c0, weight_ih, weight_hh, bias_ih, bias
     with ExitStack() as ctx:
         const = ctx.enter_context(tc.tile_pool(name="const", bufs=1))
         xpool = ctx.enter_context(tc.tile_pool(name="xpool", bufs=XB))
-        gpool = ctx.enter_context(tc.tile_pool(name="gpool", bufs=2))
-        qpool = ctx.enter_context(tc.tile_pool(name="qpool", bufs=3))
-        tpool = ctx.enter_context(tc.tile_pool(name="tpool", bufs=LEAD))
-        apool = ctx.enter_context(tc.tile_pool(name="apool", bufs=4))
+        gpool = ctx.enter_context(tc.tile_pool(name="gpool", bufs=GRPB))
+        qpool = ctx.enter_context(tc.tile_pool(name="qpool", bufs=CODB))
+        tpool = ctx.enter_context(tc.tile_pool(name="tpool", bufs=TMPB))
+        apool = ctx.enter_context(tc.tile_pool(name="apool", bufs=ACTB))
         opool = ctx.enter_context(tc.tile_pool(name="opool", bufs=4))
-        lpool = ctx.enter_context(tc.tile_pool(name="lpool", bufs=1))
-        hpool = ctx.enter_context(tc.tile_pool(name="hpool", bufs=3))
-        ps_x = ctx.enter_context(tc.psum_pool(name="ps_x", bufs=4))
-        ps_g = ctx.enter_context(tc.psum_pool(name="ps_g", bufs=2))
-        ps_p = ctx.enter_context(tc.psum_pool(name="ps_p", bufs=2))
+        lpool = ctx.enter_context(tc.tile_pool(name="lpool", bufs=3))
+        hpool = ctx.enter_context(tc.tile_pool(name="hpool", bufs=HTB))
+        ps_x = ctx.enter_context(tc.psum_pool(name="ps_x", bufs=X_BANKS))
+        ps_g = ctx.enter_context(tc.psum_pool(name="ps_g", bufs=G_BANKS))
+        ps_p = ctx.enter_context(tc.psum_pool(name="ps_p", bufs=P_BANKS))
         ctx.enter_context(tc.manual_schedule())
-
-        eng = {"v": nc.vector, "g": nc.gpsimd}
-
-        ident_f = const.tile([P, P], F32, name="ident_f")
-        ident_b = const.tile([P, P], BF16, name="ident_b")
-        make_identity(nc, ident_b[:])
-        make_identity(nc, ident_f[:])
-        btile = const.tile([P, GATES], BF16, name="btile")
-        nc.vector.memset(btile[:], 0.0)
-        ones = const.tile([P, P], BF16, name="ones")
-        nc.vector.memset(ones[:], 1.0)
-        warm = const.tile([P, 1], F32, name="warm")
-        nc.vector.memset(warm[:], 0.0)
-
-        nc.sync.dma_start(out=btile[0:1, :], in_=bias_ih.rearrange("(o n) -> o n", o=1))
-        nc.scalar.dma_start(out=btile[1:2, :], in_=bias_hh.rearrange("(o n) -> o n", o=1))
-        nc.scalar.activation(out=warm[:], in_=warm[:], func=ACT.Sigmoid)
 
         h0_parts = []
         c0_parts = []
+        xs = {}
 
         def load_part(parts, view, lo, hi, nm):
             part = const.tile([P, hi - lo, HID], BF16, name="%s%d" % (nm, lo))
@@ -105,120 +119,142 @@ def tile_symlstmcell_t_kernel(tc, x, h0, c0, weight_ih, weight_hh, bias_ih, bias
             a, part = found[0]
             return part[:, lo - a:lo - a + n, :]
 
-        xs = {}
+        def load_x(q, pieces):
+            if q not in xs:
+                xc = xpool.tile([P, 4, K_IN], BF16, name="xc")
+                xs[q] = xc
+            for lo, hi in pieces:
+                nc.sync.dma_start(out=xs[q][:, lo:hi, :], in_=xv[:, 4 * q + lo:4 * q + hi, :])
 
-        def load_x(c):
-            xc = xpool.tile([P, XC, K_IN], BF16, name="xc")
-            nc.sync.dma_start(out=xc[:], in_=xv[:, XC * c:XC * (c + 1), :])
-            xs[c] = xc
-
-        load_part(h0_parts, h0v, 0, 16, "h0p")
+        w_raw = const.tile([P, 2, 4 * GATES], BF16, name="w_raw")
+        wsrc = weight_ih.rearrange("(g p t) c -> p g (t c)", g=2, t=4)
         whh = const.tile([P, GATES], BF16, name="whh")
+
+        btile = const.tile([P, GATES], BF16, name="btile")
+        nc.vector.memset(btile[:], 0.0)
+        ident_b = const.tile([P, P], BF16, name="ident_b")
+        ident_f = const.tile([P, P], F32, name="ident_f")
+        make_identity(nc, ident_b[:])
+        make_identity(nc, ident_f[:])
+        ones = const.tile([P, P], BF16, name="ones")
+        nc.vector.memset(ones[:], 1.0)
+        warm = const.tile([P, 1], F32, name="warm")
+        nc.vector.memset(warm[:], 0.0)
+        nc.scalar.activation(out=warm[:], in_=warm[:], func=ACT.Sigmoid)
+        nc.scalar.dma_start(out=btile[0:1, :], in_=bias_ih.rearrange("(o n) -> o n", o=1))
+        nc.scalar.dma_start(out=btile[1:2, :], in_=bias_hh.rearrange("(o n) -> o n", o=1))
+
+        load_part(h0_parts, h0v, 0, 4, "h0p")
+        load_x(0, [(0, 1)])
         nc.sync.dma_start(out=whh[:], in_=weight_hh)
-        w_raw = const.tile([P, 4 * K_IN], BF16, name="w_raw")
-        nc.sync.dma_start(
-            out=w_raw[:].rearrange("p (g r) -> p g r", g=2),
-            in_=weight_ih.rearrange("(g q j) c -> q g (j c)", g=2, j=4),
-        )
-        load_x(0)
-        load_x(1)
+        load_x(0, [(1, 2)])
+        load_part(h0_parts, h0v, 4, 8, "h0p")
+        load_x(0, [(2, 3), (3, 4)])
+        for g in range(2):
+            nc.sync.dma_start(out=w_raw[:, g, :], in_=wsrc[:, g, :])
+        load_x(1, [(0, 2), (2, 4)])
+        load_part(h0_parts, h0v, 8, 16, "h0p")
+        load_x(2, [(0, 4)])
         load_part(c0_parts, c0v, 0, 16, "c0p")
-        load_x(2)
+        load_x(3, [(0, 4)])
         load_part(h0_parts, h0v, 16, NT, "h0p")
-        load_x(3)
         load_part(c0_parts, c0v, 16, NT, "c0p")
-        for c in range(4, XB):
-            load_x(c)
 
-        hT = {}
-        h0ts = {}
-        xts = {}
-        grps = {}
-        cods = {}
-        scls = {}
-        ppss = {}
-        gpss = {}
-        tmps = {}
-        acts = {}
-        c1os = {}
-        tcbs = {}
-        NQ = NT // 4
-
-        batches = []
-        j0 = 0
-        while j0 < NG:
-            n = EB if j0 + EB <= NG - TAILB else 1
-            batches.append((j0, n, SMALL if n == EB else SMALL_TAIL))
-            j0 += n
+        hT, h0ts, xts, grps, cods, scls, ppss, gpss, tmps, acts, c1os, links = {}, {}, {}, {}, {}, {}, {}, {}, {}, {}, {}, {}
+        unit_of = {}
+        for u, (lo, n) in enumerate(UNITS):
+            for t in range(lo, lo + n):
+                unit_of[t] = u
         batch_of = {}
-        for bi, (bj, bn, be) in enumerate(batches):
-            for j in range(bj, bj + bn):
-                batch_of[j] = bi
-        n_full = len([b for b in batches if b[1] == EB])
+        for b, (lo, n) in enumerate(BATCHES):
+            for t in range(lo, lo + n):
+                batch_of[t] = b
+        eng = {"V": nc.vector, "G": nc.gpsimd}
+        bias_bc = const.tile([P, GATES], F32, name="bias_bc")
+        wq = const.tile([P, 2, GATES], U32, name="wq", align_bytes=64)
+        ws = const.tile([P, 2, GATES], U8, name="ws", align_bytes=64)
+        wg0 = const.tile([P, GATES, 4], BF16, name="wg0", align_bytes=64)
+        wg1 = const.tile([P, GATES, 4], BF16, name="wg1", align_bytes=64)
+        wg = [wg0, wg1]
 
-        def on_scalar(t):
-            return t % SB_MOD in SB_SET
+        def st_BB(e, i):
+            bps = ps_p.tile([P, GATES], F32, name="pps")
+            nc.tensor.matmul(out=bps[:], lhsT=ones[:], rhs=btile[:], start=True, stop=True)
+            nc.vector.tensor_copy(out=bias_bc[:], in_=bps[:])
 
-        def st_H(b):
-            h0t = ps_x.tile([P, 8, HID], BF16, name="xt")
-            blk = part_of(h0_parts, 8 * b, 8)
-            for i in range(8):
+        def st_W(e, i):
+            dst = wg[i][:].rearrange("p (c i) t -> p c t i", i=4)
+            src = w_raw[:, i, :].rearrange("p (t c i) -> p c t i", t=4, i=4)
+            if e == "V":
+                nc.vector.tensor_copy(out=dst, in_=src)
+            elif e == "S":
+                nc.scalar.copy(out=dst, in_=src)
+            else:
+                nc.gpsimd.tensor_scalar(out=dst, in0=src, scalar1=1.0, scalar2=0.0, op0=ALU.mult, op1=ALU.add)
+
+        def st_WQ(e, i):
+            nc.vector.quantize_mx(out=wq[:, i, :].bitcast(FP8X4), scales=ws[:, i, :], in_=wg[i][:].rearrange("p c t -> p (c t)"))
+
+        def st_H(e, q):
+            h0t = ps_x.tile([P, 4, P], BF16, name="xt")
+            blk = part_of(h0_parts, 4 * q, 4)
+            for i in range(4):
                 nc.tensor.transpose(h0t[:, i, :], blk[:, i, :], ident_b[:])
-            h0ts[b] = h0t
+            h0ts[q] = h0t
 
-        def st_HC(b):
-            ht = hpool.tile([P, 8, HID], BF16, name="ht")
-            nc.scalar.copy(out=ht[:], in_=h0ts[b][:])
-            hT[b] = ht
+        def st_HC(e, q):
+            ht = hpool.tile([P, 4, HID], BF16, name="ht")
+            nc.scalar.copy(out=ht[:], in_=h0ts[q][:])
+            hT[q] = ht
 
-        def st_P(t):
+        def st_P(e, t):
             pps = ps_p.tile([P, GATES], F32, name="pps")
             sc = on_scalar(t)
-            nc.tensor.matmul(out=pps[:], lhsT=hT[t // 8][:, t % 8, :], rhs=whh[:], start=True, stop=not sc)
+            nc.tensor.matmul(out=pps[:], lhsT=hT[t // 4][:, t % 4, :], rhs=whh[:], start=True, stop=not sc)
             if sc:
                 nc.tensor.matmul(out=pps[:], lhsT=ones[:], rhs=btile[:], start=False, stop=True)
             ppss[t] = pps
 
-        def st_B(t):
-            if t // GT not in tmps:
-                tmp = tpool.tile([P, GT, GATES], F32, name="tmp")
-                tmps[t // GT] = tmp
-            dst = tmps[t // GT][:, t % GT, :]
-            if on_scalar(t):
+        def st_B(e, t):
+            if t // 2 not in tmps:
+                tmp = tpool.tile([P, 2, GATES], F32, name="tmp")
+                tmps[t // 2] = tmp
+            dst = tmps[t // 2][:, t % 2, :]
+            if e == "S":
                 nc.scalar.copy(out=dst, in_=ppss[t][:])
             else:
                 nc.vector.tensor_tensor(out=dst, in0=ppss[t][:], in1=bias_bc[:], op=ALU.add)
 
-        def st_T(t):
+        def st_T(e, t):
             xt = ps_x.tile([P, 4, P], F32, name="xt")
-            xw = xs[t // XC][:, t % XC, :].bitcast(F32)
+            xw = xs[t // 4][:, t % 4, :].bitcast(F32)
             for u in range(4):
                 lo = 2 * P * (u // 2) + u % 2
                 nc.tensor.transpose(xt[:, u, :], xw[:, lo:lo + 2 * P - 1:2], ident_f[:])
             xts[t] = xt
-            if t % XC == XC - 1 and t // XC + XB < NT // XC:
-                load_x(t // XC + XB)
+            if t % 4 == 3 and t // 4 + XB < NQ:
+                load_x(t // 4 + XB, [(0, 4)])
 
-        def st_E(t):
+        def st_E(e, t):
             q = t // 4
             if q not in grps:
                 grp = gpool.tile([P, 4, K_IN], BF16, name="grp", align_bytes=64)
                 grps[q] = grp
-            nc.scalar.copy(
-                out=grps[q][:, t % 4, :].bitcast(F32).rearrange("p (g b u) -> p g b u", g=2, u=2),
-                in_=xts[t][:].rearrange("p (g u) b -> p g b u", u=2),
-            )
+            dst = grps[q][:, t % 4, :].bitcast(F32).rearrange("p (g b u) -> p g b u", g=2, u=2)
+            src = xts[t][:].rearrange("p (g u) b -> p g b u", u=2)
+            if e == "S":
+                nc.scalar.copy(out=dst, in_=src)
+            else:
+                nc.vector.tensor_copy(out=dst, in_=src)
 
-        def st_Q(q):
+        def st_Q(e, q):
             cod = qpool.tile([P, 4 * 256], U32, name="cod", align_bytes=64)
             scl = qpool.tile([P, 4 * 256], U8, name="scl", align_bytes=64)
-            nc.vector.quantize_mx(
-                out=cod[:].bitcast(FP8X4), scales=scl[:], in_=grps[q][:].rearrange("p j c -> p (j c)")
-            )
+            nc.vector.quantize_mx(out=cod[:].bitcast(FP8X4), scales=scl[:], in_=grps[q][:].rearrange("p j c -> p (j c)"))
             cods[q] = cod
             scls[q] = scl
 
-        def st_M(t):
+        def st_M(e, t):
             gps = ps_g.tile([P, GATES], F32, name="gps")
             for g in range(2):
                 lo = (t % 4) * 256 + g * P
@@ -233,151 +269,107 @@ def tile_symlstmcell_t_kernel(tc, x, h0, c0, weight_ih, weight_hh, bias_ih, bias
                 )
             gpss[t] = gps
 
-        def st_A(t):
-            dst = tmps[t // GT][:, t % GT, :]
+        def st_A(e, t):
+            dst = tmps[t // 2][:, t % 2, :]
             nc.vector.tensor_tensor(out=dst, in0=gpss[t][:], in1=dst, op=ALU.add)
 
-        def st_S1(j):
-            bi = batch_of[j]
-            bj, bn, be = batches[bi]
-            if bi not in acts:
-                act = apool.tile([P, bn * GT, GATES], F32, name="act")
-                acts[bi] = act
-            lo = (j - bj) * GT
-            act = acts[bi][:, lo:lo + GT, :]
-            nc.scalar.activation(out=act[:, :, HID:GATES], in_=tmps[j][:, :, HID:GATES], func=ACT.Sigmoid)
-            nc.scalar.activation(out=act[:, :, 0:HID], in_=tmps[j][:, :, 0:HID], func=ACT.Tanh)
+        def st_S1(e, u):
+            lo, n = UNITS[u]
+            b = batch_of[lo]
+            blo, bn = BATCHES[b]
+            if b not in acts:
+                act = apool.tile([P, bn, GATES], F32, name="act")
+                acts[b] = act
+            act = acts[b][:, lo - blo:lo - blo + n, :]
+            src = tmps[lo // 2][:, lo % 2:lo % 2 + n, :]
+            nc.scalar.activation(out=act[:, :, HID:GATES], in_=src[:, :, HID:GATES], func=ACT.Sigmoid)
+            nc.scalar.activation(out=act[:, :, 0:HID], in_=src[:, :, 0:HID], func=ACT.Tanh)
 
-        def st_G1(bi):
-            bj, bn, be = batches[bi]
-            act = acts[bi]
-            if bn == EB:
-                m1 = lpool.tile([P, bn * GT, HID], F32, name="lk", bufs=LINKB)
-            else:
-                m1 = lpool.tile([P, bn * GT, HID], F32, name="lkt", bufs=2)
-            tcbs[bi] = m1
-            eng[be[0]].tensor_tensor(out=m1[:], in0=act[:, :, 0:HID], in1=act[:, :, HID:2 * HID], op=ALU.mult)
-            eng[be[1]].tensor_tensor(
-                out=act[:, :, 2 * HID:3 * HID], in0=act[:, :, 2 * HID:3 * HID],
-                in1=part_of(c0_parts, GT * bj, GT * bn), op=ALU.mult
-            )
+        def st_m1(e, b):
+            lo, n = BATCHES[b]
+            lk = lpool.tile([P, n, HID], F32, name="lk")
+            links[b] = lk
+            eng[e].tensor_tensor(out=lk[:], in0=acts[b][:, :, 0:HID], in1=acts[b][:, :, HID:2 * HID], op=ALU.mult)
 
-        def st_C1(bi):
-            bj, bn, be = batches[bi]
-            c1o = opool.tile([P, bn * GT, HID], F32, name="c1o")
-            c1os[bi] = c1o
-            eng[be[2]].tensor_tensor(out=c1o[:], in0=tcbs[bi][:], in1=acts[bi][:, :, 2 * HID:3 * HID], op=ALU.add)
-            nc.sync.dma_start(out=c1v[:, GT * bj:GT * (bj + bn), :], in_=c1o[:])
+        def st_cf(e, b):
+            lo, n = BATCHES[b]
+            f = acts[b][:, :, 2 * HID:3 * HID]
+            eng[e].tensor_tensor(out=f, in0=f, in1=part_of(c0_parts, lo, n), op=ALU.mult)
 
-        def st_S2(bi):
-            nc.scalar.activation(out=tcbs[bi][:], in_=c1os[bi][:], func=ACT.Tanh)
+        def st_c1(e, b):
+            lo, n = BATCHES[b]
+            c1o = opool.tile([P, n, HID], F32, name="c1o")
+            c1os[b] = c1o
+            eng[e].tensor_tensor(out=c1o[:], in0=links[b][:], in1=acts[b][:, :, 2 * HID:3 * HID], op=ALU.add)
+            nc.sync.dma_start(out=c1v[:, lo:lo + n, :], in_=c1o[:])
 
-        def st_G2(bi):
-            bj, bn, be = batches[bi]
-            h1o = opool.tile([P, bn * GT, HID], F32, name="h1o")
-            eng[be[3]].tensor_tensor(out=h1o[:], in0=tcbs[bi][:], in1=acts[bi][:, :, 3 * HID:GATES], op=ALU.mult)
-            nc.sync.dma_start(out=h1v[:, GT * bj:GT * (bj + bn), :], in_=h1o[:])
+        def st_S2(e, b):
+            nc.scalar.activation(out=links[b][:], in_=c1os[b][:], func=ACT.Tanh)
 
-        bps = ps_p.tile([P, GATES], F32, name="pps")
-        nc.tensor.matmul(out=bps[:], lhsT=ones[:], rhs=btile[:], start=True, stop=True)
-        bias_bc = const.tile([P, GATES], F32, name="bias_bc")
-        nc.vector.tensor_copy(out=bias_bc[:], in_=bps[:])
-        wview = w_raw[:].rearrange("p (g t c) -> p g t c", g=2, t=4)
-        wq = const.tile([P, 2, GATES], U32, name="wq", align_bytes=64)
-        ws = const.tile([P, 2, GATES], U8, name="ws", align_bytes=64)
-        wg0 = const.tile([P, GATES, 4], BF16, name="wg0", align_bytes=64)
-        wg1 = const.tile([P, GATES, 4], BF16, name="wg1", align_bytes=64)
+        def st_h1(e, b):
+            lo, n = BATCHES[b]
+            h1o = opool.tile([P, n, HID], F32, name="h1o")
+            eng[e].tensor_tensor(out=h1o[:], in0=links[b][:], in1=acts[b][:, :, 3 * HID:GATES], op=ALU.mult)
+            nc.sync.dma_start(out=h1v[:, lo:lo + n, :], in_=h1o[:])
 
-        def st_W(i):
-            if i == 0:
-                nc.vector.tensor_copy(
-                    out=wg0[:].rearrange("p (c i) t -> p c t i", i=4), in_=wview[:, 0].rearrange("p t (c i) -> p c t i", i=4)
-                )
-            elif i == 1:
-                nc.scalar.copy(
-                    out=wg1[:].rearrange("p (c i) t -> p c t i", i=4), in_=wview[:, 1].rearrange("p t (c i) -> p c t i", i=4)
-                )
-            elif i == 2:
-                nc.vector.quantize_mx(out=wq[:, 0, :].bitcast(FP8X4), scales=ws[:, 0, :], in_=wg0[:].rearrange("p c t -> p (c t)"))
-            else:
-                nc.vector.quantize_mx(out=wq[:, 1, :].bitcast(FP8X4), scales=ws[:, 1, :], in_=wg1[:].rearrange("p c t -> p (c t)"))
+        run = {"BB": st_BB, "W": st_W, "WQ": st_WQ, "H": st_H, "HC": st_HC, "P": st_P, "B": st_B, "T": st_T, "E": st_E, "Q": st_Q, "M": st_M,
+               "A": st_A, "S1": st_S1, "m1": st_m1, "cf": st_cf, "c1": st_c1, "S2": st_S2, "h1": st_h1}
+
+        lists = engine_lists()
+        xring = [it for it in lists["PE"] if it[0] in ("T", "H")]
+        pring = [it for it in lists["PE"] if it[0] == "P"]
+        out_of = {"T": "E", "H": "HC", "P": "B"}
+        before = {}
+        for ring, depth in ((xring, X_BANKS), (pring, P_BANKS)):
+            for n in range(depth, len(ring)):
+                before[ring[n]] = (out_of[ring[n - depth][0]], ring[n - depth][1])
 
         def needs(s, i):
+            r = [before[(s, i)]] if (s, i) in before else []
             if s == "E":
-                return [("T", i)]
-            if s == "Q":
-                return [("E", 4 * i + r) for r in range(4)]
-            if s == "M":
-                return [("Q", i // 4), ("W", 2), ("W", 3)]
-            if s == "W":
-                return [("W", i - 2)] if i >= 2 else []
-            if s == "A":
-                return [("M", i), ("B", i)]
-            if s == "B":
-                return [("P", i)]
-            if s == "P":
-                return [("HC", i // 8)]
-            if s == "HC":
-                return [("H", i)]
-            if s == "S1":
-                return [("A", GT * i), ("A", GT * i + 1)]
-            if s == "G1":
-                bj, bn, be = batches[i]
-                old = [("G2", i - LINKB)] if (bn == EB and i >= LINKB) else []
-                return [("S1", j) for j in range(bj, bj + bn)] + old
-            if s == "C1":
-                return [("G1", i)]
-            if s == "S2":
-                return [("C1", i)]
-            if s == "G2":
-                return [("S2", i)]
-            return []
-
-        count = {"T": NT, "E": NT, "Q": NQ, "M": NT, "A": NT, "B": NT, "P": NT, "H": NT // 8, "HC": NT // 8,
-                 "S1": NG, "G1": n_full, "C1": n_full, "S2": n_full, "G2": n_full, "W": 4}
-        per = {"T": 4, "E": 4, "Q": 1, "M": 4, "A": 4, "B": 4, "P": 4, "S1": 2, "G1": 1, "C1": 1, "S2": 1, "G2": 1}
-        run = {"T": st_T, "E": st_E, "Q": st_Q, "M": st_M, "A": st_A, "B": st_B, "P": st_P, "H": st_H, "HC": st_HC,
-               "S1": st_S1, "G1": st_G1, "C1": st_C1, "S2": st_S2, "G2": st_G2, "W": st_W}
-
-        def expand(order, mine):
-            out = []
-            for k in range(KH, KT):
-                for (s, ahead, r) in order:
-                    if s == "W":
-                        if k == ahead:
-                            out.append((s, r))
-                        continue
-                    if s == "H" or s == "HC":
-                        if (k + ahead) % 2 == r and 0 <= (k + ahead) // 2 < count[s]:
-                            out.append((s, (k + ahead) // 2))
-                        continue
-                    i = per[s] * (k + ahead) + r
-                    if 0 <= k + ahead and 0 <= i < count[s] and mine(s, i):
-                        if s == "S1" and batches[batch_of[i]][1] != EB:
-                            continue
-                        out.append((s, i))
-            return out
-
-        lists = [
-            HEAD[0] + expand(PE_ORDER, lambda s, i: True) + TAIL[0],
-            HEAD[1] + expand(V_ORDER, lambda s, i: s != "B" or not on_scalar(i)) + TAIL[1],
-            HEAD[2] + expand(S_ORDER, lambda s, i: s != "B" or on_scalar(i)) + TAIL[2],
-            HEAD[3] + expand(G_ORDER, lambda s, i: True) + TAIL[3],
-        ]
+                r = r + [("T", i)] + ([("Q", i // 4 - GRPB)] if i // 4 >= GRPB else [])
+            elif s == "HC":
+                r = r + [("H", i)] + (t4("P", i - HTB) if i >= HTB else [])
+            elif s == "Q":
+                r = r + t4("E", i) + (t4("M", i - CODB) if i >= CODB else [])
+            elif s == "P":
+                r = r + [("HC", i // 4)]
+            elif s == "B":
+                r = r + [("P", i), ("BB", 0)] + ([("S1", unit_of[2 * (i // 2 - TMPB) + 1])] if i // 2 >= TMPB else [])
+            elif s == "WQ":
+                r = r + [("W", i)]
+            elif s == "M":
+                r = r + [("Q", i // 4), ("WQ", 0), ("WQ", 1)] + ([("A", i - G_BANKS)] if i >= G_BANKS else [])
+            elif s == "A":
+                r = r + [("M", i), ("B", i)]
+            elif s == "S1":
+                lo, n = UNITS[i]
+                b = batch_of[lo]
+                r = r + [("A", t) for t in range(lo, lo + n)] + ([("h1", b - ACTB)] if b >= ACTB else [])
+            elif s == "m1" or s == "cf":
+                lo, n = BATCHES[i]
+                r = r + [("S1", unit_of[t]) for t in range(lo, lo + n)] + ([("h1", i - 3)] if i >= 3 else [])
+            elif s == "c1":
+                r = r + [("m1", i), ("cf", i)]
+            elif s == "S2":
+                r = r + [("c1", i)]
+            elif s == "h1":
+                r = r + [("S2", i)]
+            return r
 
         done = set()
-        pos = [0, 0, 0, 0]
-        left = sum([len(li) for li in lists])
+        pos = {e: 0 for e in lists}
+        left = sum([len(li) for li in lists.values()])
         while left > 0:
             moved = False
-            for e in range(4):
+            for e in lists:
                 while pos[e] < len(lists[e]):
                     s, i = lists[e][pos[e]]
                     if not all([d in done for d in needs(s, i)]):
                         break
-                    run[s](i)
+                    run[s](e, i)
                     done.add((s, i))
                     pos[e] += 1
                     left -= 1
                     moved = True
-            assert moved, "the orders wait for each other"
+            assert moved, "the orders wait for each other: %s" % [lists[e][pos[e]] for e in lists if pos[e] < len(lists[e])]

@@ -24,7 +24,7 @@ XB = 4
 GRPB = 2
 CODB = 3
 TMPB = 10
-ACTB = 4
+ACTB = 5
 HTB = 3
 X_BANKS, P_BANKS, G_BANKS = 4, 2, 2
 
@@ -43,15 +43,15 @@ def on_scalar(t):
 
 
 tpl = {
-    "PE": [("M", 1, 2), ("M", 1, 3), ("P", 2, 3), ("M", 2, 0), ("M", 2, 1), ("P", 3, 0), ("T", 3, 3), ("P", 3, 1), ("H", 5, 0), ("T", 4, 0), ("T", 4, 1), ("T", 4, 2), ("P", 3, 2)],
-    "V": [("A", 1, 2), ("A", 1, 3), ("B", 2, 2), ("A", 2, 0), ("A", 2, 1), ("B", 3, 0), ("h1", -1, 0), ("Q", 3, 0), ("B", 3, 1)],
-    "S": [("S1", 1, 0), ("E", 3, 1), ("S2", -1, 0), ("HC", 4, 0), ("B", 2, 3), ("E", 3, 2), ("E", 3, 3), ("S1", 1, 1), ("E", 4, 0)],
+    "PE": [("T", 2, 0), ("T", 2, 1), ("P", 1, 0), ("M", 0, 0), ("M", 0, 1), ("P", 1, 1), ("H", 2, 0), ("T", 2, 2), ("T", 2, 3), ("P", 1, 2), ("M", 0, 2), ("M", 0, 3), ("P", 1, 3)],
+    "V": [("A", -1, 2), ("A", -1, 3), ("h1", -3, 0), ("Q", 1, 0), ("B", 1, 0), ("A", 0, 0), ("A", 0, 1), ("B", 1, 1), ("B", 1, 2)],
+    "S": [("E", 2, 0), ("S2", -2, 0), ("E", 2, 1), ("HC", 2, 0), ("E", 2, 2), ("E", 2, 3), ("S1", 0, 0), ("B", 1, 3), ("S1", 0, 1)],
     "G": [("m1", 1, 0), ("cf", 1, 0), ("c1", 1, 0)],
 }
 head = {
-    "PE": [("H", 0), ("T", 0), ("P", 0), ("T", 1), ("P", 1), ("T", 2), ("P", 2), ("T", 3), ("H", 1), ("P", 3), ("T", 4), ("P", 4), ("T", 5), ("P", 5), ("M", 0), ("M", 1), ("T", 6), ("T", 7)],
-    "V": [("BB", 0), ("B", 0), ("B", 1), ("B", 2), ("W", 0), ("WQ", 0), ("Q", 0), ("B", 4), ("WQ", 1), ("A", 0), ("B", 5), ("Q", 1)],
-    "S": [("HC", 0)]+t4("E", 0)+[("HC", 1), ("B", 3), ("W", 1), ("E", 4), ("E", 5), ("E", 6), ("E", 7)],
+    "PE": [("H", 0), ("T", 0), ("P", 0), ("T", 1), ("P", 1), ("H", 1), ("T", 2), ("P", 2), ("T", 3), ("P", 3), ("T", 4), ("T", 5), ("T", 6), ("T", 7), ("M", 0), ("M", 1), ("P", 4), ("P", 5)],
+    "V": [("BB", 0), ("B", 0), ("B", 1), ("W", 0), ("W", 1), ("WQ", 0), ("WQ", 1), ("Q", 0), ("B", 2), ("Q", 1), ("A", 0), ("A", 1), ("B", 4), ("B", 5)],
+    "S": [("HC", 0), ("E", 0), ("E", 1), ("HC", 1), ("E", 2), ("E", 3), ("B", 3), ("E", 4), ("E", 5)],
     "G": [],
 }
 tail = {
@@ -158,7 +158,6 @@ def tile_symlstmcell_t_kernel(tc, x, h0, c0, weight_ih, weight_hh, bias_ih, bias
         load_part(c0_parts, c0v, 0, 16, "c0p")
         load_x(3, [(0, 4)])
         load_part(h0_parts, h0v, 16, NT, "h0p")
-        load_part(c0_parts, c0v, 16, NT, "c0p")
 
         hT, h0ts, xts, grps, cods, scls, ppss, gpss, tmps, acts, c1os, links = {}, {}, {}, {}, {}, {}, {}, {}, {}, {}, {}, {}
         unit_of = {}
@@ -234,6 +233,8 @@ def tile_symlstmcell_t_kernel(tc, x, h0, c0, weight_ih, weight_hh, bias_ih, bias
             xts[t] = xt
             if t % 4 == 3 and t // 4 + XB < NQ:
                 load_x(t // 4 + XB, [(0, 4)])
+                if t == 3:
+                    load_part(c0_parts, c0v, 16, NT, "c0p")
 
         def st_E(e, t):
             q = t // 4

@@ -20,6 +20,7 @@ NT = BATCH // P
 NQ = NT // 4
 FLOPS = 2 * BATCH * K_IN * GATES + 2 * BATCH * HID * GATES
 
+SEQ = "W"
 XB = 4
 GRPB = 2
 CODB = 3
@@ -28,8 +29,8 @@ ACTB = 5
 HTB = 3
 X_BANKS, P_BANKS, G_BANKS = 4, 2, 2
 
-BATCHES = [(4 * q, 4) for q in range(NQ - 1)] + [(60, 2), (62, 1), (63, 1)]
-UNITS = [(2 * u, 2) for u in range(2 * NQ - 2)] + [(60, 2), (62, 1), (63, 1)]
+BATCHES = [(4 * q, 4) for q in range(NQ - 1)] + [(60, 2), (62, 2)]
+UNITS = [(2 * u, 2) for u in range(2 * NQ)]
 NB = NQ - 1
 NU = 2 * NQ - 2
 
@@ -38,32 +39,36 @@ def t4(s, q):
     return [(s, 4 * q + r) for r in range(4)]
 
 
+def small_engine(s, q):
+    return "V" if s == "h1" else "G"
+
+
 def on_scalar(t):
     return t % 4 == 3
 
 
 tpl = {
-    "PE": [("T", 2, 0), ("T", 2, 1), ("P", 1, 0), ("M", 0, 0), ("M", 0, 1), ("P", 1, 1), ("H", 2, 0), ("T", 2, 2), ("T", 2, 3), ("P", 1, 2), ("M", 0, 2), ("M", 0, 3), ("P", 1, 3)],
-    "V": [("A", -1, 2), ("A", -1, 3), ("h1", -3, 0), ("Q", 1, 0), ("B", 1, 0), ("A", 0, 0), ("A", 0, 1), ("B", 1, 1), ("B", 1, 2)],
-    "S": [("E", 2, 0), ("S2", -2, 0), ("E", 2, 1), ("HC", 2, 0), ("E", 2, 2), ("E", 2, 3), ("S1", 0, 0), ("B", 1, 3), ("S1", 0, 1)],
-    "G": [("m1", 1, 0), ("cf", 1, 0), ("c1", 1, 0)],
+    "PE": [("P", 0, 2), ("M", 0, 0), ("M", 0, 1), ("P", 0, 3), ("H", 2, 0), ("P", 1, 0), ("M", 0, 2), ("M", 0, 3), ("P", 1, 1), ("T", 2, 0), ("T", 2, 1), ("T", 2, 2), ("T", 2, 3)],
+    "V": [("B", 0, 2), ("A", 0, 0), ("A", 0, 1), ("B", 1, 0), ("A", 0, 2), ("A", 0, 3), ("Q", 1, 0), ("h1", -2, 0), ("B", 1, 1)],
+    "S": [("B", 0, 3), ("HC", 2, 0), ("S1", 0, 0), ("S1", 0, 1), ("E", 2, 0), ("E", 2, 1), ("E", 2, 2), ("E", 2, 3), ("S2", -1, 0)],
+    "G": [("cf", 0, 0), ("m1", 0, 0), ("c1", 0, 0)],
 }
 head = {
-    "PE": [("H", 0), ("T", 0), ("P", 0), ("T", 1), ("P", 1), ("H", 1), ("T", 2), ("P", 2), ("T", 3), ("P", 3), ("T", 4), ("T", 5), ("T", 6), ("T", 7), ("M", 0), ("M", 1), ("P", 4), ("P", 5)],
-    "V": [("BB", 0), ("B", 0), ("B", 1), ("W", 0), ("W", 1), ("WQ", 0), ("WQ", 1), ("Q", 0), ("B", 2), ("Q", 1), ("A", 0), ("A", 1), ("B", 4), ("B", 5)],
-    "S": [("HC", 0), ("E", 0), ("E", 1), ("HC", 1), ("E", 2), ("E", 3), ("B", 3), ("E", 4), ("E", 5)],
+    "PE": [("H", 0), ("T", 0), ("P", 0), ("T", 1), ("P", 1), ("T", 2), ("T", 3), ("H", 1), ("T", 4), ("T", 5), ("T", 6), ("T", 7)],
+    "V": [("BB", 0), ("B", 0), ("W", 0), ("W", 1), ("WQ", 0), ("WQ", 1), ("Qh", 0), ("B", 1), ("Qh", 1)],
+    "S": [("HC", 0), ("E", 0), ("E", 1), ("E", 2), ("E", 3), ("HC", 1), ("E", 4), ("E", 5), ("E", 6), ("E", 7)],
     "G": [],
 }
 tail = {
-    "PE": [],"V": [("cf", 14), ("m1", 15), ("cf", 15), ("c1", 14), ("c1", 15), ("m1", 16), ("cf", 16), ("h1", 14), ("c1", 16), ("h1", 15), ("m1", 17), ("cf", 17), ("c1", 17), ("h1", 16), ("h1", 17)],
-    "S": [("S1", 30), ("S1", 31), ("S2", 14), ("S1", 32), ("S2", 15), ("S2", 16), ("S2", 17)],"G": []
+    "PE": [],"V": [("h1", 13), ("m1", 15), ("cf", 15), ("c1", 15), ("m1", 16), ("cf", 16), ("c1", 16), ("h1", 14), ("h1", 15), ("h1", 16)],
+    "S": [("S1", 30), ("S1", 31), ("S2", 14), ("S2", 15), ("S2", 16)],"G": []
 }
 
 
 def engine_lists():
     per = {"T": 4, "E": 4, "M": 4, "A": 4, "P": 4, "B": 4, "Q": 1, "S1": 2, "S2": 1, "m1": 1, "cf": 1, "c1": 1, "h1": 1, "H": 1, "HC": 1}
     count = {"T": NT, "E": NT, "M": NT, "A": NT, "P": NT, "B": NT, "Q": NQ, "S1": NU, "S2": NB, "m1": NB, "cf": NB, "c1": NB, "h1": NB, "H": NQ, "HC": NQ}
-    placed = set()
+    placed = {("Q", 0)}
     for e in tpl:
         placed = placed | set(head[e]) | set(tail[e])
     lists = {}
@@ -75,6 +80,8 @@ def engine_lists():
                 if k + a < 0 or i >= count[s] or (s, i) in placed:
                     continue
                 if s == "B" and (e == "S") != on_scalar(i):
+                    continue
+                if s in ("m1", "cf", "c1", "h1") and e != small_engine(s, i):
                     continue
                 lst.append((s, i))
         lists[e] = lst + tail[e]
@@ -148,10 +155,10 @@ def tile_symlstmcell_t_kernel(tc, x, h0, c0, weight_ih, weight_hh, bias_ih, bias
         load_x(0, [(0, 1)])
         nc.sync.dma_start(out=whh[:], in_=weight_hh)
         load_x(0, [(1, 2)])
-        load_part(h0_parts, h0v, 4, 8, "h0p")
-        load_x(0, [(2, 3), (3, 4)])
         for g in range(2):
             nc.sync.dma_start(out=w_raw[:, g, :], in_=wsrc[:, g, :])
+        load_x(0, [(2, 3), (3, 4)])
+        load_part(h0_parts, h0v, 4, 8, "h0p")
         load_x(1, [(0, 2), (2, 4)])
         load_part(h0_parts, h0v, 8, 16, "h0p")
         load_x(2, [(0, 4)])
@@ -203,7 +210,10 @@ def tile_symlstmcell_t_kernel(tc, x, h0, c0, weight_ih, weight_hh, bias_ih, bias
 
         def st_HC(e, q):
             ht = hpool.tile([P, 4, HID], BF16, name="ht")
-            nc.scalar.copy(out=ht[:], in_=h0ts[q][:])
+            if e == "S":
+                nc.scalar.copy(out=ht[:], in_=h0ts[q][:])
+            else:
+                nc.vector.tensor_copy(out=ht[:], in_=h0ts[q][:])
             hT[q] = ht
 
         def st_P(e, t):
@@ -254,6 +264,18 @@ def tile_symlstmcell_t_kernel(tc, x, h0, c0, weight_ih, weight_hh, bias_ih, bias
             nc.vector.quantize_mx(out=cod[:].bitcast(FP8X4), scales=scl[:], in_=grps[q][:].rearrange("p j c -> p (j c)"))
             cods[q] = cod
             scls[q] = scl
+
+        def st_Qh(e, i):
+            if 0 not in cods:
+                cod = qpool.tile([P, 4 * 256], U32, name="cod", align_bytes=64)
+                scl = qpool.tile([P, 4 * 256], U8, name="scl", align_bytes=64)
+                cods[0] = cod
+                scls[0] = scl
+            src = grps[0][:].rearrange("p j c -> p (j c)")
+            lo = 512 * i
+            nc.vector.quantize_mx(
+                out=cods[0][:, lo:lo + 512].bitcast(FP8X4), scales=scls[0][:, lo:lo + 512], in_=src[:, 4 * lo:4 * lo + 2048]
+            )
 
         def st_M(e, t):
             gps = ps_g.tile([P, GATES], F32, name="gps")
@@ -313,7 +335,7 @@ def tile_symlstmcell_t_kernel(tc, x, h0, c0, weight_ih, weight_hh, bias_ih, bias
             eng[e].tensor_tensor(out=h1o[:], in0=links[b][:], in1=acts[b][:, :, 3 * HID:GATES], op=ALU.mult)
             nc.sync.dma_start(out=h1v[:, lo:lo + n, :], in_=h1o[:])
 
-        run = {"BB": st_BB, "W": st_W, "WQ": st_WQ, "H": st_H, "HC": st_HC, "P": st_P, "B": st_B, "T": st_T, "E": st_E, "Q": st_Q, "M": st_M,
+        run = {"BB": st_BB, "W": st_W, "WQ": st_WQ, "H": st_H, "HC": st_HC, "P": st_P, "B": st_B, "T": st_T, "E": st_E, "Q": st_Q, "Qh": st_Qh, "M": st_M,
                "A": st_A, "S1": st_S1, "m1": st_m1, "cf": st_cf, "c1": st_c1, "S2": st_S2, "h1": st_h1}
 
         lists = engine_lists()
@@ -328,9 +350,11 @@ def tile_symlstmcell_t_kernel(tc, x, h0, c0, weight_ih, weight_hh, bias_ih, bias
         def needs(s, i):
             r = [before[(s, i)]] if (s, i) in before else []
             if s == "E":
-                r = r + [("T", i)] + ([("Q", i // 4 - GRPB)] if i // 4 >= GRPB else [])
+                r = r + [("T", i)] + ([("Qh", 1) if i // 4 == GRPB else ("Q", i // 4 - GRPB)] if i // 4 >= GRPB else [])
             elif s == "HC":
                 r = r + [("H", i)] + (t4("P", i - HTB) if i >= HTB else [])
+            elif s == "Qh":
+                r = r + [("E", 2 * i), ("E", 2 * i + 1)]
             elif s == "Q":
                 r = r + t4("E", i) + (t4("M", i - CODB) if i >= CODB else [])
             elif s == "P":
@@ -340,7 +364,7 @@ def tile_symlstmcell_t_kernel(tc, x, h0, c0, weight_ih, weight_hh, bias_ih, bias
             elif s == "WQ":
                 r = r + [("W", i)]
             elif s == "M":
-                r = r + [("Q", i // 4), ("WQ", 0), ("WQ", 1)] + ([("A", i - G_BANKS)] if i >= G_BANKS else [])
+                r = r + [("Qh", i // 2) if i < 4 else ("Q", i // 4), ("WQ", 0), ("WQ", 1)] + ([("A", i - G_BANKS)] if i >= G_BANKS else [])
             elif s == "A":
                 r = r + [("M", i), ("B", i)]
             elif s == "S1":

@@ -21,6 +21,7 @@ NQ = NT // 4
 FLOPS = 2 * BATCH * K_IN * GATES + 2 * BATCH * HID * GATES
 
 SEQ = "W"
+W_CUT = 352
 XB = 4
 GRPB = 2
 CODB = 3
@@ -54,9 +55,9 @@ tpl = {
     "G": [("cf", 0, 0), ("m1", 0, 0), ("c1", 0, 0)],
 }
 head = {
-    "PE": [("H", 0), ("T", 0), ("P", 0), ("T", 1), ("P", 1), ("T", 2), ("T", 3), ("H", 1), ("T", 4), ("T", 5), ("T", 6), ("T", 7)],
+    "PE": [("H", 0), ("T", 0), ("P", 0), ("T", 1), ("P", 1), ("T", 2), ("T", 3), ("H", 1), ("P", 2), ("T", 4), ("T", 5), ("M", 0), ("M", 1), ("P", 3), ("T", 6), ("P", 4), ("M", 2), ("M", 3), ("T", 7), ("P", 5), ("H", 2)],
     "V": [("BB", 0), ("B", 0), ("W", 0), ("W", 1), ("WQ", 0), ("WQ", 1), ("Qh", 0), ("B", 1), ("Qh", 1)],
-    "S": [("HC", 0), ("E", 0), ("E", 1), ("E", 2), ("E", 3), ("HC", 1), ("E", 4), ("E", 5), ("E", 6), ("E", 7)],
+    "S": [("HC", 0), ("E", 0), ("E", 1), ("Wb", 0), ("Wb", 1), ("E", 2), ("E", 3), ("HC", 1), ("E", 4), ("E", 5), ("B", 3), ("E", 6), ("S1", 0), ("E", 7), ("HC", 2)],
     "G": [],
 }
 tail = {
@@ -148,11 +149,11 @@ def tile_symlstmcell_t_kernel(tc, x, h0, c0, weight_ih, weight_hh, bias_ih, bias
         warm = const.tile([P, 1], F32, name="warm")
         nc.vector.memset(warm[:], 0.0)
         nc.scalar.activation(out=warm[:], in_=warm[:], func=ACT.Sigmoid)
-        nc.scalar.dma_start(out=btile[0:1, :], in_=bias_ih.rearrange("(o n) -> o n", o=1))
-        nc.scalar.dma_start(out=btile[1:2, :], in_=bias_hh.rearrange("(o n) -> o n", o=1))
 
         load_part(h0_parts, h0v, 0, 4, "h0p")
         load_x(0, [(0, 1)])
+        nc.sync.dma_start(out=btile[0:1, :], in_=bias_ih.rearrange("(o n) -> o n", o=1))
+        nc.sync.dma_start(out=btile[1:2, :], in_=bias_hh.rearrange("(o n) -> o n", o=1))
         nc.sync.dma_start(out=whh[:], in_=weight_hh)
         load_x(0, [(1, 2)])
         for g in range(2):
@@ -188,15 +189,17 @@ def tile_symlstmcell_t_kernel(tc, x, h0, c0, weight_ih, weight_hh, bias_ih, bias
             nc.tensor.matmul(out=bps[:], lhsT=ones[:], rhs=btile[:], start=True, stop=True)
             nc.vector.tensor_copy(out=bias_bc[:], in_=bps[:])
 
+        def regroup_w(engine_copy, i, lo, hi):
+            engine_copy(
+                out=wg[i][:, lo:hi, :].rearrange("p (c i) t -> p c t i", i=4),
+                in_=w_raw[:, i, :].rearrange("p (t c i) -> p c t i", t=4, i=4)[:, lo // 4:hi // 4],
+            )
+
         def st_W(e, i):
-            dst = wg[i][:].rearrange("p (c i) t -> p c t i", i=4)
-            src = w_raw[:, i, :].rearrange("p (t c i) -> p c t i", t=4, i=4)
-            if e == "V":
-                nc.vector.tensor_copy(out=dst, in_=src)
-            elif e == "S":
-                nc.scalar.copy(out=dst, in_=src)
-            else:
-                nc.gpsimd.tensor_scalar(out=dst, in0=src, scalar1=1.0, scalar2=0.0, op0=ALU.mult, op1=ALU.add)
+            regroup_w(nc.vector.tensor_copy, i, 0, W_CUT)
+
+        def st_Wb(e, i):
+            regroup_w(nc.scalar.copy, i, W_CUT, GATES)
 
         def st_WQ(e, i):
             nc.vector.quantize_mx(out=wq[:, i, :].bitcast(FP8X4), scales=ws[:, i, :], in_=wg[i][:].rearrange("p c t -> p (c t)"))
@@ -335,7 +338,7 @@ def tile_symlstmcell_t_kernel(tc, x, h0, c0, weight_ih, weight_hh, bias_ih, bias
             eng[e].tensor_tensor(out=h1o[:], in0=links[b][:], in1=acts[b][:, :, 3 * HID:GATES], op=ALU.mult)
             nc.sync.dma_start(out=h1v[:, lo:lo + n, :], in_=h1o[:])
 
-        run = {"BB": st_BB, "W": st_W, "WQ": st_WQ, "H": st_H, "HC": st_HC, "P": st_P, "B": st_B, "T": st_T, "E": st_E, "Q": st_Q, "Qh": st_Qh, "M": st_M,
+        run = {"BB": st_BB, "W": st_W, "Wb": st_Wb, "WQ": st_WQ, "H": st_H, "HC": st_HC, "P": st_P, "B": st_B, "T": st_T, "E": st_E, "Q": st_Q, "Qh": st_Qh, "M": st_M,
                "A": st_A, "S1": st_S1, "m1": st_m1, "cf": st_cf, "c1": st_c1, "S2": st_S2, "h1": st_h1}
 
         lists = engine_lists()
@@ -362,7 +365,7 @@ def tile_symlstmcell_t_kernel(tc, x, h0, c0, weight_ih, weight_hh, bias_ih, bias
             elif s == "B":
                 r = r + [("P", i), ("BB", 0)] + ([("S1", unit_of[2 * (i // 2 - TMPB) + 1])] if i // 2 >= TMPB else [])
             elif s == "WQ":
-                r = r + [("W", i)]
+                r = r + [("W", i), ("Wb", i)]
             elif s == "M":
                 r = r + [("Qh", i // 2) if i < 4 else ("Q", i // 4), ("WQ", 0), ("WQ", 1)] + ([("A", i - G_BANKS)] if i >= G_BANKS else [])
             elif s == "A":

from contextlib import ExitStack

import concourse.mybir as mybir
from concourse.masks import make_identity

F32 = mybir.dt.float32
BF16 = mybir.dt.bfloat16
U32 = mybir.dt.uint32
U8 = mybir.dt.uint8
FP8X4 = mybir.dt.float8_e4m3fn_x4
ACT = mybir.ActivationFunctionType
ALU = mybir.AluOpType

P = 128
BATCH = 8192
K_IN = 1024
HID = 128
GATES = 512
NT = BATCH // P
NQ = NT // 4
FLOPS = 2 * BATCH * K_IN * GATES + 2 * BATCH * HID * GATES

SEQ = "W"
W_CUT = 352
XB = 4
GRPB = 2
CODB = 3
TMPB = 10
ACTB = 5
HTB = 3
X_BANKS, P_BANKS, G_BANKS = 4, 2, 2

BATCHES = [(4 * q, 4) for q in range(NQ - 1)] + [(60, 2), (62, 2)]
UNITS = [(2 * u, 2) for u in range(2 * NQ)]
NB = NQ - 1
NU = 2 * NQ - 2


def t4(s, q):
    return [(s, 4 * q + r) for r in range(4)]


def small_engine(s, q):
    return "V" if s == "h1" else "G"


def on_scalar(t):
    return t % 4 == 3


tpl = {
    "PE": [("P", 0, 2), ("M", 0, 0), ("M", 0, 1), ("P", 0, 3), ("H", 2, 0), ("P", 1, 0), ("M", 0, 2), ("M", 0, 3), ("P", 1, 1), ("T", 2, 0), ("T", 2, 1), ("T", 2, 2), ("T", 2, 3)],
    "V": [("B", 0, 2), ("A", 0, 0), ("A", 0, 1), ("B", 1, 0), ("A", 0, 2), ("A", 0, 3), ("Q", 1, 0), ("h1", -2, 0), ("B", 1, 1)],
    "S": [("B", 0, 3), ("HC", 2, 0), ("S1", 0, 0), ("S1", 0, 1), ("E", 2, 0), ("E", 2, 1), ("E", 2, 2), ("E", 2, 3), ("S2", -1, 0)],
    "G": [("cf", 0, 0), ("m1", 0, 0), ("c1", 0, 0)],
}
head = {
    "PE": [("H", 0), ("T", 0), ("P", 0), ("T", 1), ("P", 1), ("T", 2), ("T", 3), ("H", 1), ("P", 2), ("T", 4), ("T", 5), ("M", 0), ("M", 1), ("P", 3), ("T", 6), ("P", 4), ("M", 2), ("M", 3), ("T", 7), ("P", 5), ("H", 2)],
    "V": [("BB", 0), ("B", 0), ("W", 0), ("W", 1), ("WQ", 0), ("WQ", 1), ("Qh", 0), ("B", 1), ("Qh", 1)],
    "S": [("HC", 0), ("E", 0), ("E", 1), ("Wb", 0), ("Wb", 1), ("E", 2), ("E", 3), ("HC", 1), ("E", 4), ("E", 5), ("B", 3), ("E", 6), ("S1", 0), ("E", 7), ("HC", 2)],
    "G": [],
}
tail = {
    "PE": [],"V": [("h1", 13), ("m1", 15), ("cf", 15), ("c1", 15), ("m1", 16), ("cf", 16), ("c1", 16), ("h1", 14), ("h1", 15), ("h1", 16)],
    "S": [("S1", 30), ("S1", 31), ("S2", 14), ("S2", 15), ("S2", 16)],"G": []
}


def engine_lists():
    per = {"T": 4, "E": 4, "M": 4, "A": 4, "P": 4, "B": 4, "Q": 1, "S1": 2, "S2": 1, "m1": 1, "cf": 1, "c1": 1, "h1": 1, "H": 1, "HC": 1}
    count = {"T": NT, "E": NT, "M": NT, "A": NT, "P": NT, "B": NT, "Q": NQ, "S1": NU, "S2": NB, "m1": NB, "cf": NB, "c1": NB, "h1": NB, "H": NQ, "HC": NQ}
    placed = {("Q", 0)}
    for e in tpl:
        placed = placed | set(head[e]) | set(tail[e])
    lists = {}
    for e in tpl:
        lst = list(head[e])
        for k in range(-8, NQ + 8):
            for s, a, r in tpl[e]:
                i = per[s] * (k + a) + r
                if k + a < 0 or i >= count[s] or (s, i) in placed:
                    continue
                if s == "B" and (e == "S") != on_scalar(i):
                    continue
                if s in ("m1", "cf", "c1", "h1") and e != small_engine(s, i):
                    continue
                lst.append((s, i))
        lists[e] = lst + tail[e]
    return lists


def tile_symlstmcell_t_kernel(tc, x, h0, c0, weight_ih, weight_hh, bias_ih, bias_hh, out_0, out_1):
    nc = tc.nc
    xv = x.rearrange("(p t) k -> p t k", t=NT)
    h0v = h0.rearrange("(p t) k -> p t k", t=NT)
    c0v = c0.rearrange("(p t) k -> p t k", t=NT)
    h1v = out_0.rearrange("(p t) u -> p t u", t=NT)
    c1v = out_1.rearrange("(p t) u -> p t u", t=NT)

    with ExitStack() as ctx:
        const = ctx.enter_context(tc.tile_pool(name="const", bufs=1))
        xpool = ctx.enter_context(tc.tile_pool(name="xpool", bufs=XB))
        gpool = ctx.enter_context(tc.tile_pool(name="gpool", bufs=GRPB))
        qpool = ctx.enter_context(tc.tile_pool(name="qpool", bufs=CODB))
        tpool = ctx.enter_context(tc.tile_pool(name="tpool", bufs=TMPB))
        apool = ctx.enter_context(tc.tile_pool(name="apool", bufs=ACTB))
        opool = ctx.enter_context(tc.tile_pool(name="opool", bufs=4))
        lpool = ctx.enter_context(tc.tile_pool(name="lpool", bufs=3))
        hpool = ctx.enter_context(tc.tile_pool(name="hpool", bufs=HTB))
        ps_x = ctx.enter_context(tc.psum_pool(name="ps_x", bufs=X_BANKS))
        ps_g = ctx.enter_context(tc.psum_pool(name="ps_g", bufs=G_BANKS))
        ps_p = ctx.enter_context(tc.psum_pool(name="ps_p", bufs=P_BANKS))
        ctx.enter_context(tc.manual_schedule())

        h0_parts = []
        c0_parts = []
        xs = {}

        def load_part(parts, view, lo, hi, nm):
            part = const.tile([P, hi - lo, HID], BF16, name="%s%d" % (nm, lo))
            nc.sync.dma_start(out=part[:], in_=view[:, lo:hi, :])
            parts.append((lo, hi, part))

        def part_of(parts, lo, n):
            found = [(a, part) for (a, b, part) in parts if a <= lo and lo + n <= b]
            assert len(found) == 1
            a, part = found[0]
            return part[:, lo - a:lo - a + n, :]

        def load_x(q, pieces):
            if q not in xs:
                xc = xpool.tile([P, 4, K_IN], BF16, name="xc")
                xs[q] = xc
            for lo, hi in pieces:
                nc.sync.dma_start(out=xs[q][:, lo:hi, :], in_=xv[:, 4 * q + lo:4 * q + hi, :])

        w_raw = const.tile([P, 2, 4 * GATES], BF16, name="w_raw")
        wsrc = weight_ih.rearrange("(g p t) c -> p g (t c)", g=2, t=4)
        whh = const.tile([P, GATES], BF16, name="whh")

        btile = const.tile([P, GATES], BF16, name="btile")
        nc.vector.memset(btile[:], 0.0)
        ident_b = const.tile([P, P], BF16, name="ident_b")
        ident_f = const.tile([P, P], F32, name="ident_f")
        make_identity(nc, ident_b[:])
        make_identity(nc, ident_f[:])
        ones = const.tile([P, P], BF16, name="ones")
        nc.vector.memset(ones[:], 1.0)
        warm = const.tile([P, 1], F32, name="warm")
        nc.vector.memset(warm[:], 0.0)
        nc.scalar.activation(out=warm[:], in_=warm[:], func=ACT.Sigmoid)

        load_part(h0_parts, h0v, 0, 4, "h0p")
        load_x(0, [(0, 1)])
        nc.sync.dma_start(out=btile[0:1, :], in_=bias_ih.rearrange("(o n) -> o n", o=1))
        nc.sync.dma_start(out=btile[1:2, :], in_=bias_hh.rearrange("(o n) -> o n", o=1))
        nc.sync.dma_start(out=whh[:], in_=weight_hh)
        load_x(0, [(1, 2)])
        for g in range(2):
            nc.sync.dma_start(out=w_raw[:, g, :], in_=wsrc[:, g, :])
        load_x(0, [(2, 3), (3, 4)])
        load_part(h0_parts, h0v, 4, 8, "h0p")
        load_x(1, [(0, 2), (2, 4)])
        load_part(h0_parts, h0v, 8, 16, "h0p")
        load_x(2, [(0, 4)])
        load_part(c0_parts, c0v, 0, 16, "c0p")
        load_x(3, [(0, 4)])
        load_part(h0_parts, h0v, 16, NT, "h0p")

        hT, h0ts, xts, grps, cods, scls, ppss, gpss, tmps, acts, c1os, links = {}, {}, {}, {}, {}, {}, {}, {}, {}, {}, {}, {}
        unit_of = {}
        for u, (lo, n) in enumerate(UNITS):
            for t in range(lo, lo + n):
                unit_of[t] = u
        batch_of = {}
        for b, (lo, n) in enumerate(BATCHES):
            for t in range(lo, lo + n):
                batch_of[t] = b
        eng = {"V": nc.vector, "G": nc.gpsimd}
        bias_bc = const.tile([P, GATES], F32, name="bias_bc")
        wq = const.tile([P, 2, GATES], U32, name="wq", align_bytes=64)
        ws = const.tile([P, 2, GATES], U8, name="ws", align_bytes=64)
        wg0 = const.tile([P, GATES, 4], BF16, name="wg0", align_bytes=64)
        wg1 = const.tile([P, GATES, 4], BF16, name="wg1", align_bytes=64)
        wg = [wg0, wg1]

        def st_BB(e, i):
            bps = ps_p.tile([P, GATES], F32, name="pps")
            nc.tensor.matmul(out=bps[:], lhsT=ones[:], rhs=btile[:], start=True, stop=True)
            nc.vector.tensor_copy(out=bias_bc[:], in_=bps[:])

        def regroup_w(engine_copy, i, lo, hi):
            engine_copy(
                out=wg[i][:, lo:hi, :].rearrange("p (c i) t -> p c t i", i=4),
                in_=w_raw[:, i, :].rearrange("p (t c i) -> p c t i", t=4, i=4)[:, lo // 4:hi // 4],
            )

        def st_W(e, i):
            regroup_w(nc.vector.tensor_copy, i, 0, W_CUT)

        def st_Wb(e, i):
            regroup_w(nc.scalar.copy, i, W_CUT, GATES)

        def st_WQ(e, i):
            nc.vector.quantize_mx(out=wq[:, i, :].bitcast(FP8X4), scales=ws[:, i, :], in_=wg[i][:].rearrange("p c t -> p (c t)"))

        def st_H(e, q):
            h0t = ps_x.tile([P, 4, P], BF16, name="xt")
            blk = part_of(h0_parts, 4 * q, 4)
            for i in range(4):
                nc.tensor.transpose(h0t[:, i, :], blk[:, i, :], ident_b[:])
            h0ts[q] = h0t

        def st_HC(e, q):
            ht = hpool.tile([P, 4, HID], BF16, name="ht")
            if e == "S":
                nc.scalar.copy(out=ht[:], in_=h0ts[q][:])
            else:
                nc.vector.tensor_copy(out=ht[:], in_=h0ts[q][:])
            hT[q] = ht

        def st_P(e, t):
            pps = ps_p.tile([P, GATES], F32, name="pps")
            sc = on_scalar(t)
            nc.tensor.matmul(out=pps[:], lhsT=hT[t // 4][:, t % 4, :], rhs=whh[:], start=True, stop=not sc)
            if sc:
                nc.tensor.matmul(out=pps[:], lhsT=ones[:], rhs=btile[:], start=False, stop=True)
            ppss[t] = pps

        def st_B(e, t):
            if t // 2 not in tmps:
                tmp = tpool.tile([P, 2, GATES], F32, name="tmp")
                tmps[t // 2] = tmp
            dst = tmps[t // 2][:, t % 2, :]
            if e == "S":
                nc.scalar.copy(out=dst, in_=ppss[t][:])
            else:
                nc.vector.tensor_tensor(out=dst, in0=ppss[t][:], in1=bias_bc[:], op=ALU.add)

        def st_T(e, t):
            xt = ps_x.tile([P, 4, P], F32, name="xt")
            xw = xs[t // 4][:, t % 4, :].bitcast(F32)
            for u in range(4):
                lo = 2 * P * (u // 2) + u % 2
                nc.tensor.transpose(xt[:, u, :], xw[:, lo:lo + 2 * P - 1:2], ident_f[:])
            xts[t] = xt
            if t % 4 == 3 and t // 4 + XB < NQ:
                load_x(t // 4 + XB, [(0, 4)])
                if t == 3:
                    load_part(c0_parts, c0v, 16, NT, "c0p")

        def st_E(e, t):
            q = t // 4
            if q not in grps:
                grp = gpool.tile([P, 4, K_IN], BF16, name="grp", align_bytes=64)
                grps[q] = grp
            dst = grps[q][:, t % 4, :].bitcast(F32).rearrange("p (g b u) -> p g b u", g=2, u=2)
            src = xts[t][:].rearrange("p (g u) b -> p g b u", u=2)
            if e == "S":
                nc.scalar.copy(out=dst, in_=src)
            else:
                nc.vector.tensor_copy(out=dst, in_=src)

        def st_Q(e, q):
            cod = qpool.tile([P, 4 * 256], U32, name="cod", align_bytes=64)
            scl = qpool.tile([P, 4 * 256], U8, name="scl", align_bytes=64)
            nc.vector.quantize_mx(out=cod[:].bitcast(FP8X4), scales=scl[:], in_=grps[q][:].rearrange("p j c -> p (j c)"))
            cods[q] = cod
            scls[q] = scl

        def st_Qh(e, i):
            if 0 not in cods:
                cod = qpool.tile([P, 4 * 256], U32, name="cod", align_bytes=64)
                scl = qpool.tile([P, 4 * 256], U8, name="scl", align_bytes=64)
                cods[0] = cod
                scls[0] = scl
            src = grps[0][:].rearrange("p j c -> p (j c)")
            lo = 512 * i
            nc.vector.quantize_mx(
                out=cods[0][:, lo:lo + 512].bitcast(FP8X4), scales=scls[0][:, lo:lo + 512], in_=src[:, 4 * lo:4 * lo + 2048]
            )

        def st_M(e, t):
            gps = ps_g.tile([P, GATES], F32, name="gps")
            for g in range(2):
                lo = (t % 4) * 256 + g * P
                nc.tensor.matmul_mx(
                    out=gps[:],
                    lhsT=cods[t // 4][:, lo:lo + P].bitcast(FP8X4),
                    lhsT_scale=scls[t // 4][:, lo:lo + P],
                    rhs=wq[:, g, :].bitcast(FP8X4),
                    rhs_scale=ws[:, g, :],
                    start=(g == 0),
                    stop=(g == 1),
                )
            gpss[t] = gps

        def st_A(e, t):
            dst = tmps[t // 2][:, t % 2, :]
            nc.vector.tensor_tensor(out=dst, in0=gpss[t][:], in1=dst, op=ALU.add)

        def st_S1(e, u):
            lo, n = UNITS[u]
            b = batch_of[lo]
            blo, bn = BATCHES[b]
            if b not in acts:
                act = apool.tile([P, bn, GATES], F32, name="act")
                acts[b] = act
            act = acts[b][:, lo - blo:lo - blo + n, :]
            src = tmps[lo // 2][:, lo % 2:lo % 2 + n, :]
            nc.scalar.activation(out=act[:, :, HID:GATES], in_=src[:, :, HID:GATES], func=ACT.Sigmoid)
            nc.scalar.activation(out=act[:, :, 0:HID], in_=src[:, :, 0:HID], func=ACT.Tanh)

        def st_m1(e, b):
            lo, n = BATCHES[b]
            lk = lpool.tile([P, n, HID], F32, name="lk")
            links[b] = lk
            eng[e].tensor_tensor(out=lk[:], in0=acts[b][:, :, 0:HID], in1=acts[b][:, :, HID:2 * HID], op=ALU.mult)

        def st_cf(e, b):
            lo, n = BATCHES[b]
            f = acts[b][:, :, 2 * HID:3 * HID]
            eng[e].tensor_tensor(out=f, in0=f, in1=part_of(c0_parts, lo, n), op=ALU.mult)

        def st_c1(e, b):
            lo, n = BATCHES[b]
            c1o = opool.tile([P, n, HID], F32, name="c1o")
            c1os[b] = c1o
            eng[e].tensor_tensor(out=c1o[:], in0=links[b][:], in1=acts[b][:, :, 2 * HID:3 * HID], op=ALU.add)
            nc.sync.dma_start(out=c1v[:, lo:lo + n, :], in_=c1o[:])

        def st_S2(e, b):
            nc.scalar.activation(out=links[b][:], in_=c1os[b][:], func=ACT.Tanh)

        def st_h1(e, b):
            lo, n = BATCHES[b]
            h1o = opool.tile([P, n, HID], F32, name="h1o")
            eng[e].tensor_tensor(out=h1o[:], in0=links[b][:], in1=acts[b][:, :, 3 * HID:GATES], op=ALU.mult)
            nc.sync.dma_start(out=h1v[:, lo:lo + n, :], in_=h1o[:])

        run = {"BB": st_BB, "W": st_W, "Wb": st_Wb, "WQ": st_WQ, "H": st_H, "HC": st_HC, "P": st_P, "B": st_B, "T": st_T, "E": st_E, "Q": st_Q, "Qh": st_Qh, "M": st_M,
               "A": st_A, "S1": st_S1, "m1": st_m1, "cf": st_cf, "c1": st_c1, "S2": st_S2, "h1": st_h1}

        lists = engine_lists()
        xring = [it for it in lists["PE"] if it[0] in ("T", "H")]
        pring = [it for it in lists["PE"] if it[0] == "P"]
        out_of = {"T": "E", "H": "HC", "P": "B"}
        before = {}
        for ring, depth in ((xring, X_BANKS), (pring, P_BANKS)):
            for n in range(depth, len(ring)):
                before[ring[n]] = (out_of[ring[n - depth][0]], ring[n - depth][1])

        def needs(s, i):
            r = [before[(s, i)]] if (s, i) in before else []
            if s == "E":
                r = r + [("T", i)] + ([("Qh", 1) if i // 4 == GRPB else ("Q", i // 4 - GRPB)] if i // 4 >= GRPB else [])
            elif s == "HC":
                r = r + [("H", i)] + (t4("P", i - HTB) if i >= HTB else [])
            elif s == "Qh":
                r = r + [("E", 2 * i), ("E", 2 * i + 1)]
            elif s == "Q":
                r = r + t4("E", i) + (t4("M", i - CODB) if i >= CODB else [])
            elif s == "P":
                r = r + [("HC", i // 4)]
            elif s == "B":
                r = r + [("P", i), ("BB", 0)] + ([("S1", unit_of[2 * (i // 2 - TMPB) + 1])] if i // 2 >= TMPB else [])
            elif s == "WQ":
                r = r + [("W", i), ("Wb", i)]
            elif s == "M":
                r = r + [("Qh", i // 2) if i < 4 else ("Q", i // 4), ("WQ", 0), ("WQ", 1)] + ([("A", i - G_BANKS)] if i >= G_BANKS else [])
            elif s == "A":
                r = r + [("M", i), ("B", i)]
            elif s == "S1":
                lo, n = UNITS[i]
                b = batch_of[lo]
                r = r + [("A", t) for t in range(lo, lo + n)] + ([("h1", b - ACTB)] if b >= ACTB else [])
            elif s == "m1" or s == "cf":
                lo, n = BATCHES[i]
                r = r + [("S1", unit_of[t]) for t in range(lo, lo + n)] + ([("h1", i - 3)] if i >= 3 else [])
            elif s == "c1":
                r = r + [("m1", i), ("cf", i)]
            elif s == "S2":
                r = r + [("c1", i)]
            elif s == "h1":
                r = r + [("S2", i)]
            return r

        done = set()
        pos = {e: 0 for e in lists}
        left = sum([len(li) for li in lists.values()])
        while left > 0:
            moved = False
            for e in lists:
                while pos[e] < len(lists[e]):
                    s, i = lists[e][pos[e]]
                    if not all([d in done for d in needs(s, i)]):
                        break
                    run[s](e, i)
                    done.add((s, i))
                    pos[e] += 1
                    left -= 1
                    moved = True
            assert moved, "the orders wait for each other: %s" % [lists[e][pos[e]] for e in lists if pos[e] < len(lists[e])]
